import numpy as np
import ml_dtypes


def mxq(x, axis, fmt="e4m3"):
    dtype, down = {"e4m3": (ml_dtypes.float8_e4m3fn, 7), "e5m2": (ml_dtypes.float8_e5m2, 14)}[fmt]
    v = np.moveaxis(np.asarray(x, np.float32).astype(ml_dtypes.bfloat16).astype(np.float64), axis, -1)
    blocks = v.reshape(v.shape[:-1] + (-1, 32))
    amax = np.abs(blocks).max(-1, keepdims=True)
    byte = np.maximum(np.where(amax > 0, np.frexp(amax)[1] - 1 + 127, 0) - down, 1)
    scale = np.exp2(byte - 127.0)
    codes = (blocks / scale).astype(np.float32).astype(dtype).astype(np.float64)
    return np.moveaxis((codes * scale).reshape(v.shape), -1, axis)


WIDE = False


def mx_kscale(k):
    if not WIDE:
        return np.ones(k)
    levels = np.array([10, -10, 5, -5, 0])
    a = np.random.permutation(np.resize(levels, k // 512 * 4)).reshape(k // 512, 4)
    idx = np.arange(k)
    return np.exp2(a[idx // 512, idx % 128 // 32])


BF16 = ml_dtypes.bfloat16


def bf(x):
    return np.asarray(x, np.float32).astype(BF16)


def f64(x):
    return np.asarray(x).astype(np.float64)


B, T, C, H, QB = 1, 1024, 2048, 256, 512
D = H // 2
DEPTH = 2
LAMBDA_INIT = 0.8 - 0.6 * np.exp(-0.3 * (DEPTH - 1))
LS = np.sqrt(0.15 / D)


def softmax(s):
    e = np.exp(s - s.max(-1, keepdims=True))
    return e / e.sum(-1, keepdims=True)


def setup_inputs():
    s = mx_kscale(C)
    return {"q": bf(np.random.standard_normal((B, T, H)) * 1.5),
            "k": bf(np.random.standard_normal((B, T, H)) * 1.5),
            "x": bf(np.random.standard_normal((B, T, C)) * s),
            "Wv": bf(np.random.standard_normal((H, C)) / np.sqrt(C) / s[None, :]),
            "lambda_q1": bf(LS * (1.0 + np.random.standard_normal(D))),
            "lambda_q2": bf(LS * (1.0 + np.random.standard_normal(D))),
            "lambda_k1": bf(LS * (1.0 + np.random.standard_normal(D))),
            "lambda_k2": bf(-LS * (1.0 + np.random.standard_normal(D)))}


def reference(q, k, x, Wv, lambda_q1, lambda_q2, lambda_k1, lambda_k2):
    q, k = f64(q), f64(k)
    v = mxq(f64(x), 2, "e4m3") @ mxq(f64(Wv), 1, "e4m3").T
    vq = mxq(v, 1, "e4m3")
    lam = (np.exp(np.sum(f64(lambda_q1) * f64(lambda_k1)))
           - np.exp(np.sum(f64(lambda_q2) * f64(lambda_k2)))
           + LAMBDA_INIT)
    scale = 1.0 / np.sqrt(D)
    rows = []
    for r0 in range(0, T, QB):
        r1 = r0 + QB
        causal = np.arange(r0, r1)[:, None] >= np.arange(r1)[None, :]
        s1 = q[:, r0:r1, :D] @ k[:, :r1, :D].transpose(0, 2, 1) * scale
        s2 = q[:, r0:r1, D:] @ k[:, :r1, D:].transpose(0, 2, 1) * scale
        att1 = softmax(np.where(causal, s1, -np.inf))
        att2 = softmax(np.where(causal, s2, -np.inf))
        att = att1 - lam * att2
        rows.append(mxq(att, 2, "e4m3") @ vq[:, :r1])
    return np.concatenate(rows, 1)

@@ -1,0 +1,455 @@
+import math
+from contextlib import ExitStack
+
+import concourse.mybir as mybir
+from concourse.masks import make_identity
+
+BF16 = mybir.dt.bfloat16
+F32 = mybir.dt.float32
+U32 = mybir.dt.uint32
+U8 = mybir.dt.uint8
+FP8X4 = mybir.dt.float8_e4m3fn_x4
+ALU = mybir.AluOpType
+ACT = mybir.ActivationFunctionType
+AXIS_X = mybir.AxisListType.X
+
+P = 128
+T = 1024
+C = 2048
+H = 256
+D = 128
+K_PASS = 512
+BANK = 512
+BLOCKS = T // P
+PAIRS = T // (2 * P)
+C_PASSES = C // K_PASS
+KEY_PASSES = T // K_PASS
+
+SCALE = 1.0 / math.sqrt(D)
+LAMBDA_INIT = 0.8 - 0.6 * math.exp(-0.3)
+MASKED = -1.0e30
+
+CAUSAL_PAIRS = 512 * 512 + 512 * 1024
+FLOPS = 2 * T * C * H + 2 * 2 * CAUSAL_PAIRS * D + 2 * CAUSAL_PAIRS * H
+
+
+def tile_diffattn_pa_kernel(
+    tc, q, k, x, Wv, lambda_q1, lambda_q2, lambda_k1, lambda_k2, out
+):
+    nc = tc.nc
+    q_rows = q.flatten_outer_dims()
+    k_rows = k.flatten_outer_dims()
+    x_rows = x.flatten_outer_dims()
+    out_rows = out.flatten_outer_dims()
+
+    with ExitStack() as stack:
+        keep = stack.enter_context(tc.tile_pool(name="keep", bufs=1))
+        work = stack.enter_context(tc.tile_pool(name="work", bufs=2))
+        stats = stack.enter_context(tc.tile_pool(name="stats", bufs=3))
+        psum_s = stack.enter_context(tc.psum_pool(name="psum_s", bufs=4))
+        psum_t = stack.enter_context(tc.psum_pool(name="psum_t", bufs=3))
+        psum_a = stack.enter_context(tc.psum_pool(name="psum_a", bufs=1))
+
+        k_sb = keep.tile([P, BLOCKS * H], BF16, name="k_sb")
+        q_sb = keep.tile([P, BLOCKS * H], BF16, name="q_sb")
+
+        def load_half(dst, rows, half):
+            nc.sync.dma_start(
+                out=dst[:, half * 4 * H : (half + 1) * 4 * H].rearrange("p (b d) -> p b d", d=H),
+                in_=rows[half * 512 : (half + 1) * 512, :].rearrange("(b p) d -> p b d", p=P),
+            )
+
+        load_half(k_sb, k_rows, 0)
+        load_half(k_sb, k_rows, 1)
+        load_half(q_sb, q_rows, 1)
+        load_half(q_sb, q_rows, 0)
+
+        w_sb = keep.tile([P, 2 * C], BF16, name="w_sb")
+        nc.sync.dma_start(
+            out=w_sb[:].rearrange("p (a c) -> p a c", a=2),
+            in_=Wv.rearrange("(a p) c -> p a c", p=P),
+        )
+        x_sb = [keep.tile([P, 2 * C], BF16, name="x_sb%d" % j) for j in range(PAIRS)]
+        for j in range(PAIRS):
+            nc.sync.dma_start(
+                out=x_sb[j][:],
+                in_=x_rows[j * 2 * P : (j + 1) * 2 * P, :].rearrange("(p e) c -> p (e c)", e=2),
+            )
+
+        lam_rows = keep.tile([P, P], BF16, name="lam_rows")
+        nc.vector.memset(lam_rows[:], 0.0)
+        for r, vec in enumerate((lambda_q1, lambda_q2, lambda_k1, lambda_k2)):
+            nc.scalar.dma_start(
+                out=lam_rows[r : r + 1, :], in_=vec.rearrange("(o d) -> o d", o=1)
+            )
+
+        ones_f32 = keep.tile([P, P], F32, name="ones_f32")
+        nc.vector.memset(ones_f32[:], 1.0)
+
+        warm = keep.tile([P, 1], F32, name="warm")
+        nc.scalar.activation(out=warm[:], in_=ones_f32[:, 0:1], func=ACT.Exp)
+        ident_bf = keep.tile([P, P], BF16, name="ident_bf")
+        make_identity(nc, ident_bf[:])
+        ident_f32 = keep.tile([P, P], F32, name="ident_f32")
+        make_identity(nc, ident_f32[:])
+        mask_f32 = keep.tile([P, P], F32, name="mask_f32")
+        nc.gpsimd.memset(mask_f32[:], 0.0)
+        nc.gpsimd.affine_select(
+            out=mask_f32[:],
+            in_=mask_f32[:],
+            compare_op=ALU.is_ge,
+            fill=MASKED,
+            base=0,
+            pattern=[[-1, P]],
+            channel_multiplier=1,
+        )
+        mask_bf = keep.tile([P, P], BF16, name="mask_bf")
+        nc.vector.tensor_copy(out=mask_bf[:], in_=mask_f32[:])
+
+        key_passes_of = [b // 4 + 1 for b in range(BLOCKS)]
+        att = [
+            keep.tile([P, key_passes_of[b] * K_PASS], BF16, name="att%d" % b)
+            for b in range(BLOCKS)
+        ]
+        att_grouped = [
+            keep.tile([P, key_passes_of[b] * K_PASS], BF16, name="att_grouped%d" % b, align_bytes=64)
+            for b in range(BLOCKS)
+        ]
+        att_codes = [
+            keep.tile([P, key_passes_of[b] * P], U32, name="att_codes%d" % b, align_bytes=64)
+            for b in range(BLOCKS)
+        ]
+        att_scales = [
+            keep.tile([P, key_passes_of[b] * P], U8, name="att_scales%d" % b, align_bytes=64)
+            for b in range(BLOCKS)
+        ]
+        for b in range(BLOCKS):
+            if (b + 1) * P < key_passes_of[b] * K_PASS:
+                nc.gpsimd.memset(att[b][:, (b + 1) * P :], 0.0)
+
+        kT = keep.tile([P, 2 * T], BF16, name="kT")
+        qT = keep.tile([P, 2 * T], BF16, name="qT")
+
+        def transpose_half(src, dst, half):
+            for h in range(2):
+                tp = psum_t.tile([P, BANK], BF16, tag="tp")
+                for i in range(4):
+                    b = half * 4 + i
+                    nc.tensor.transpose(
+                        tp[:, i * P : (i + 1) * P],
+                        src[:, b * H + h * D : b * H + (h + 1) * D],
+                        ident_bf[:],
+                    )
+                dst_cols = dst[:, h * T + half * 512 : h * T + (half + 1) * 512]
+                if h == 0:
+                    nc.vector.tensor_copy(out=dst_cols, in_=tp[:])
+                else:
+                    nc.scalar.copy(out=dst_cols, in_=tp[:])
+
+        neg_lam = keep.tile([P, 1], F32, name="neg_lam")
+
+        def compute_lam():
+            lam_t = psum_t.tile([P, BANK], BF16, tag="tp")
+            nc.tensor.transpose(lam_t[:, 0:P], lam_rows[:], ident_bf[:])
+            lam_cols = keep.tile([P, 4], F32, name="lam_cols")
+            nc.vector.tensor_copy(out=lam_cols[:], in_=lam_t[:, 0:4])
+            lam_prod = keep.tile([P, 2], F32, name="lam_prod")
+            nc.vector.tensor_mul(out=lam_prod[:], in0=lam_cols[:, 0:2], in1=lam_cols[:, 2:4])
+            lam_dot = psum_t.tile([P, BANK], F32, tag="tp")
+            nc.tensor.matmul(
+                lam_dot[:, 0:2], lhsT=ones_f32[:], rhs=lam_prod[:], start=True, stop=True
+            )
+            lam_exp = keep.tile([P, 2], F32, name="lam_exp")
+            nc.scalar.activation(out=lam_exp[:], in_=lam_dot[:, 0:2], func=ACT.Exp)
+            nc.vector.tensor_scalar(
+                out=neg_lam[:],
+                in0=lam_exp[:, 1:2],
+                scalar1=lam_exp[:, 0:1],
+                scalar2=LAMBDA_INIT,
+                op0=ALU.subtract,
+                op1=ALU.subtract,
+            )
+
+        def words_onto_partitions(src, grouped, c_pass):
+            src_words = src[:].bitcast(F32)
+            tp = psum_t.tile([P, BANK], F32, tag="tp")
+            for u in range(2):
+                for a in range(2):
+                    first = a * (C // 2) + (2 * c_pass + u) * P
+                    nc.tensor.transpose(
+                        tp[:, (u * 2 + a) * P : (u * 2 + a + 1) * P],
+                        src_words[:, first : first + P],
+                        ident_f32[:],
+                    )
+            dst = (
+                grouped[:]
+                .bitcast(F32)[:, c_pass * BANK : (c_pass + 1) * BANK]
+                .rearrange("p (n u) -> p n u", u=2)
+            )
+            if c_pass == C_PASSES - 1:
+                nc.vector.tensor_copy(out=dst, in_=tp[:].rearrange("p (u n) -> p n u", u=2))
+            else:
+                nc.scalar.copy(out=dst, in_=tp[:].rearrange("p (u n) -> p n u", u=2))
+
+        GROUP_WORDS = C_PASSES * 2 * P
+        w_grouped = keep.tile([P, GROUP_WORDS * 4], BF16, name="w_grouped", align_bytes=64)
+        w_codes = keep.tile([P, GROUP_WORDS], U32, name="w_codes", align_bytes=64)
+        w_scales = keep.tile([P, GROUP_WORDS], U8, name="w_scales", align_bytes=64)
+        x_grouped = [
+            keep.tile([P, GROUP_WORDS * 4], BF16, name="x_grouped%d" % j, align_bytes=64)
+            for j in range(PAIRS)
+        ]
+        x_codes = keep.tile([P, PAIRS * GROUP_WORDS], U32, name="x_codes", align_bytes=64)
+        x_scales = keep.tile([P, PAIRS * GROUP_WORDS], U8, name="x_scales", align_bytes=64)
+
+        def quantise_weight():
+            nc.vector.quantize_mx(
+                out=w_codes[:].bitcast(FP8X4), scales=w_scales[:], in_=w_grouped[:]
+            )
+
+        def quantise_x(j):
+            cols = slice(j * GROUP_WORDS, (j + 1) * GROUP_WORDS)
+            nc.vector.quantize_mx(
+                out=x_codes[:, cols].bitcast(FP8X4), scales=x_scales[:, cols], in_=x_grouped[j][:]
+            )
+
+        v_grouped = keep.tile([P, KEY_PASSES * H * 4], BF16, name="v_grouped", align_bytes=64)
+        v_codes = keep.tile([P, KEY_PASSES * H], U32, name="v_codes", align_bytes=64)
+        v_scales = keep.tile([P, KEY_PASSES * H], U8, name="v_scales", align_bytes=64)
+
+        def project_v(g):
+            for half in range(2):
+                acc = psum_t.tile([P, BANK], F32, tag="tp")
+                for t in range(4):
+                    for c_pass in range(C_PASSES):
+                        x_first = ((2 * g + t // 2) * C_PASSES + c_pass) * 2 * P + (t % 2) * P
+                        w_first = c_pass * H + half * P
+                        nc.tensor.matmul_mx(
+                            out=acc[:, t * P : (t + 1) * P],
+                            lhsT=x_codes[:, x_first : x_first + P].bitcast(FP8X4),
+                            lhsT_scale=x_scales[:, x_first : x_first + P],
+                            rhs=w_codes[:, w_first : w_first + P].bitcast(FP8X4),
+                            rhs_scale=w_scales[:, w_first : w_first + P],
+                            start=(c_pass == 0),
+                            stop=(c_pass == C_PASSES - 1),
+                        )
+                first = (g * 2 + half) * BANK
+                nc.scalar.copy(
+                    out=v_grouped[:, first : first + BANK].rearrange("p (n t) -> p n t", t=4),
+                    in_=acc[:].rearrange("p (t n) -> p n t", t=4),
+                )
+
+        def quantise_v(g):
+            nc.vector.quantize_mx(
+                out=v_codes[:, g * H : (g + 1) * H].bitcast(FP8X4),
+                scales=v_scales[:, g * H : (g + 1) * H],
+                in_=v_grouped[:, g * H * 4 : (g + 1) * H * 4],
+            )
+
+        score_banks = {}
+        stat_tiles = {}
+        exp_tiles = {}
+
+        def scores(b, h):
+            keys = (b + 1) * P
+            banks = key_passes_of[b]
+            queries = qT[:, h * T + b * P : h * T + (b + 1) * P]
+            score_banks[(b, h)] = []
+            for c in range(banks):
+                first = c * BANK
+                width = min(keys - first, BANK)
+                sc = psum_s.tile([P, BANK], F32, tag="sc")
+                score_banks[(b, h)].append((sc, first, width))
+                before = width - P if c == banks - 1 else width
+                if before > 0:
+                    nc.tensor.matmul(
+                        sc[:, 0:before],
+                        lhsT=queries,
+                        rhs=kT[:, h * T + first : h * T + first + before],
+                        start=True,
+                        stop=True,
+                    )
+                if c == banks - 1:
+                    nc.tensor.matmul(
+                        sc[:, before:width], lhsT=ident_bf[:], rhs=mask_bf[:], start=True, stop=False
+                    )
+                    nc.tensor.matmul(
+                        sc[:, before:width],
+                        lhsT=queries,
+                        rhs=kT[:, h * T + first + before : h * T + first + width],
+                        start=False,
+                        stop=True,
+                    )
+
+        def row_max(b, h):
+            if h == 0:
+                bank_max = stats.tile([P, 4], F32, tag="bank_max")
+                neg_max = stats.tile([P, 2], F32, tag="neg_max")
+                bank_sum = stats.tile([P, 4], F32, tag="bank_sum")
+                stat_tiles[b] = (bank_max, neg_max, bank_sum)
+            bank_max, neg_max, bank_sum = stat_tiles[b]
+            for c, (sc, first, width) in enumerate(score_banks[(b, h)]):
+                nc.vector.tensor_reduce(
+                    out=bank_max[:, 2 * h + c : 2 * h + c + 1],
+                    in_=sc[:, 0:width],
+                    axis=AXIS_X,
+                    op=ALU.max,
+                )
+            if key_passes_of[b] == 1:
+                nc.vector.tensor_scalar(
+                    out=neg_max[:, h : h + 1],
+                    in0=bank_max[:, 2 * h : 2 * h + 1],
+                    scalar1=-SCALE,
+                    scalar2=None,
+                    op0=ALU.mult,
+                )
+            else:
+                nc.vector.tensor_scalar(
+                    out=neg_max[:, h : h + 1],
+                    in0=bank_max[:, 2 * h : 2 * h + 1],
+                    scalar1=bank_max[:, 2 * h + 1 : 2 * h + 2],
+                    scalar2=-SCALE,
+                    op0=ALU.max,
+                    op1=ALU.mult,
+                )
+
+        def exps(b, h):
+            if h == 0:
+                expd = work.tile([P, 2 * T], F32, tag="expd")
+                exp_tiles[b] = expd
+            bank_max, neg_max, bank_sum = stat_tiles[b]
+            for c, (sc, first, width) in enumerate(score_banks[(b, h)]):
+                nc.scalar.activation(
+                    out=exp_tiles[b][:, h * T + first : h * T + first + width],
+                    in_=sc[:, 0:width],
+                    func=ACT.Exp,
+                    bias=neg_max[:, h : h + 1],
+                    scale=SCALE,
+                    accum_out=bank_sum[:, 2 * h + c : 2 * h + c + 1],
+                )
+
+        def combine(b):
+            keys = (b + 1) * P
+            bank_max, neg_max, bank_sum = stat_tiles[b]
+            expd = exp_tiles[b]
+            inv_sum = stats.tile([P, 2], F32, tag="inv_sum")
+            if key_passes_of[b] == 1:
+                nc.vector.reciprocal(out=inv_sum[:], in_=bank_sum[:, 0:4:2])
+            else:
+                row_sum = stats.tile([P, 2], F32, tag="row_sum")
+                nc.vector.tensor_reduce(
+                    out=row_sum[:],
+                    in_=bank_sum[:].rearrange("p (h c) -> p h c", c=2),
+                    axis=AXIS_X,
+                    op=ALU.add,
+                )
+                nc.vector.reciprocal(out=inv_sum[:], in_=row_sum[:])
+            second = work.tile([P, T], F32, tag="second")
+            nc.vector.tensor_scalar(
+                out=second[:, 0:keys],
+                in0=expd[:, T : T + keys],
+                scalar1=inv_sum[:, 1:2],
+                scalar2=neg_lam[:, 0:1],
+                op0=ALU.mult,
+                op1=ALU.mult,
+            )
+            nc.vector.scalar_tensor_tensor(
+                out=att[b][:, 0:keys],
+                in0=expd[:, 0:keys],
+                scalar=inv_sum[:, 0:1],
+                in1=second[:, 0:keys],
+                op0=ALU.mult,
+                op1=ALU.add,
+            )
+
+        att_banks = {}
+
+        def transpose_att(b):
+            att_words = att[b][:].bitcast(F32)
+            at = psum_a.tile([P, BANK], F32, tag="at")
+            att_banks[b] = at
+            for i in range(key_passes_of[b] * 2):
+                nc.tensor.transpose(
+                    at[:, i * P : (i + 1) * P], att_words[:, i * P : (i + 1) * P], ident_f32[:]
+                )
+
+        def regroup_att(b):
+            g = key_passes_of[b]
+            nc.scalar.copy(
+                out=att_grouped[b][:].bitcast(F32).rearrange("p (g n u) -> p g n u", g=g, u=2),
+                in_=att_banks[b][:, 0 : g * 2 * P].rearrange("p (g u n) -> p g n u", g=g, u=2),
+            )
+
+        def quantise_att(b):
+            nc.vector.quantize_mx(
+                out=att_codes[b][:].bitcast(FP8X4), scales=att_scales[b][:], in_=att_grouped[b][:]
+            )
+
+        def attention_output(b):
+            acc = psum_t.tile([P, BANK], F32, tag="tp")
+            for g in range(key_passes_of[b]):
+                nc.tensor.matmul_mx(
+                    out=acc[:, 0:H],
+                    lhsT=att_codes[b][:, g * P : (g + 1) * P].bitcast(FP8X4),
+                    lhsT_scale=att_scales[b][:, g * P : (g + 1) * P],
+                    rhs=v_codes[:, g * H : (g + 1) * H].bitcast(FP8X4),
+                    rhs_scale=v_scales[:, g * H : (g + 1) * H],
+                    start=(g == 0),
+                    stop=(g == key_passes_of[b] - 1),
+                )
+            o_sb = keep.tile([P, H], F32, name="o_sb%d" % b)
+            nc.scalar.copy(out=o_sb[:], in_=acc[:, 0:H])
+            nc.sync.dma_start(out=out_rows[b * P : (b + 1) * P, :], in_=o_sb[:])
+
+        transpose_half(k_sb, kT, 0)
+        transpose_half(k_sb, kT, 1)
+        transpose_half(q_sb, qT, 1)
+        scores(BLOCKS - 1, 0)
+        scores(BLOCKS - 1, 1)
+        finished = []
+        for step in range(BLOCKS + 2):
+            cur, mid, old = BLOCKS - 1 - step, BLOCKS - step, BLOCKS + 1 - step
+            if cur >= 0:
+                for h in range(2):
+                    row_max(cur, h)
+                    exps(cur, h)
+            if 0 <= old < BLOCKS:
+                regroup_att(old)
+            if step == 1:
+                quantise_weight()
+            if step in (2, 3):
+                quantise_x(2 * step - 4)
+                quantise_x(2 * step - 3)
+            if step in (3, 4):
+                quantise_v(step - 3)
+            if 0 <= old < BLOCKS:
+                quantise_att(old)
+                finished.append(old)
+            if 0 <= mid < BLOCKS:
+                combine(mid)
+            if step == 0:
+                pieces = [(w_sb, w_grouped)]
+            elif step in (1, 2):
+                pieces = [(x_sb[j], x_grouped[j]) for j in (2 * step - 2, 2 * step - 1)]
+            else:
+                pieces = []
+            units = [(src, dst, c_pass) for (src, dst) in pieces for c_pass in range(C_PASSES)]
+            if cur >= 1:
+                scores(cur - 1, 0)
+            if step == 0:
+                transpose_half(q_sb, qT, 0)
+                compute_lam()
+            for src, dst, c_pass in units[0:2]:
+                words_onto_partitions(src, dst, c_pass)
+            if cur >= 1:
+                scores(cur - 1, 1)
+            for src, dst, c_pass in units[2:]:
+                words_onto_partitions(src, dst, c_pass)
+            if step in (2, 3):
+                project_v(step - 2)
+            if 0 <= mid < BLOCKS:
+                transpose_att(mid)
+            if step >= 4:
+                for b in finished:
+                    attention_output(b)
+                finished = []

@@ -53,16 +53,16 @@ def tile_diffattn_pa_kernel(
         k_sb = keep.tile([P, BLOCKS * H], BF16, name="k_sb")
         q_sb = keep.tile([P, BLOCKS * H], BF16, name="q_sb")
 
-        def load_half(dst, rows, half):
+        def load_blocks(dst, rows, first, count):
             nc.sync.dma_start(
-                out=dst[:, half * 4 * H : (half + 1) * 4 * H].rearrange("p (b d) -> p b d", d=H),
-                in_=rows[half * 512 : (half + 1) * 512, :].rearrange("(b p) d -> p b d", p=P),
+                out=dst[:, first * H : (first + count) * H].rearrange("p (b d) -> p b d", d=H),
+                in_=rows[first * P : (first + count) * P, :].rearrange("(b p) d -> p b d", p=P),
             )
 
-        load_half(k_sb, k_rows, 0)
-        load_half(k_sb, k_rows, 1)
-        load_half(q_sb, q_rows, 1)
-        load_half(q_sb, q_rows, 0)
+        load_blocks(q_sb, q_rows, 6, 2)
+        load_blocks(k_sb, k_rows, 0, 4)
+        load_blocks(k_sb, k_rows, 4, 4)
+        load_blocks(q_sb, q_rows, 4, 2)
 
         w_sb = keep.tile([P, 2 * C], BF16, name="w_sb")
         nc.sync.dma_start(
@@ -75,6 +75,8 @@ def tile_diffattn_pa_kernel(
                 out=x_sb[j][:],
                 in_=x_rows[j * 2 * P : (j + 1) * 2 * P, :].rearrange("(p e) c -> p (e c)", e=2),
             )
+        load_blocks(q_sb, q_rows, 2, 2)
+        load_blocks(q_sb, q_rows, 0, 2)
 
         lam_rows = keep.tile([P, P], BF16, name="lam_rows")
         nc.vector.memset(lam_rows[:], 0.0)
@@ -130,21 +132,36 @@ def tile_diffattn_pa_kernel(
         kT = keep.tile([P, 2 * T], BF16, name="kT")
         qT = keep.tile([P, 2 * T], BF16, name="qT")
 
-        def transpose_half(src, dst, half):
+        def transpose_keys(half):
             for h in range(2):
                 tp = psum_t.tile([P, BANK], BF16, tag="tp")
                 for i in range(4):
                     b = half * 4 + i
                     nc.tensor.transpose(
                         tp[:, i * P : (i + 1) * P],
-                        src[:, b * H + h * D : b * H + (h + 1) * D],
+                        k_sb[:, b * H + h * D : b * H + (h + 1) * D],
                         ident_bf[:],
                     )
-                dst_cols = dst[:, h * T + half * 512 : h * T + (half + 1) * 512]
+                dst_cols = kT[:, h * T + half * 512 : h * T + (half + 1) * 512]
                 if h == 0:
                     nc.vector.tensor_copy(out=dst_cols, in_=tp[:])
                 else:
                     nc.scalar.copy(out=dst_cols, in_=tp[:])
+
+        def transpose_queries(pair):
+            tp = psum_t.tile([P, BANK], BF16, tag="tp")
+            for h in range(2):
+                for i in range(2):
+                    b = 2 * pair + i
+                    nc.tensor.transpose(
+                        tp[:, (2 * h + i) * P : (2 * h + i + 1) * P],
+                        q_sb[:, b * H + h * D : b * H + (h + 1) * D],
+                        ident_bf[:],
+                    )
+            nc.vector.tensor_copy(
+                out=qT[:].rearrange("p (h t) -> p h t", h=2)[:, :, 2 * pair * P : (2 * pair + 2) * P],
+                in_=tp[:].rearrange("p (h t) -> p h t", h=2),
+            )
 
         neg_lam = keep.tile([P, 1], F32, name="neg_lam")
 
@@ -401,9 +418,9 @@ def tile_diffattn_pa_kernel(
             nc.scalar.copy(out=o_sb[:], in_=acc[:, 0:H])
             nc.sync.dma_start(out=out_rows[b * P : (b + 1) * P, :], in_=o_sb[:])
 
-        transpose_half(k_sb, kT, 0)
-        transpose_half(k_sb, kT, 1)
-        transpose_half(q_sb, qT, 1)
+        transpose_queries(3)
+        transpose_keys(0)
+        transpose_keys(1)
         scores(BLOCKS - 1, 0)
         scores(BLOCKS - 1, 1)
         finished = []
@@ -437,8 +454,9 @@ def tile_diffattn_pa_kernel(
             if cur >= 1:
                 scores(cur - 1, 0)
             if step == 0:
-                transpose_half(q_sb, qT, 0)
                 compute_lam()
+            if step in (0, 2, 4):
+                transpose_queries(2 - step // 2)
             for src, dst, c_pass in units[0:2]:
                 words_onto_partitions(src, dst, c_pass)
             if cur >= 1:

@@ -59,8 +59,9 @@ def tile_diffattn_pa_kernel(
                 in_=rows[first * P : (first + count) * P, :].rearrange("(b p) d -> p b d", p=P),
             )
 
-        load_blocks(q_sb, q_rows, 6, 2)
+        load_blocks(q_sb, q_rows, 2, 2)
         load_blocks(k_sb, k_rows, 0, 4)
+        load_blocks(q_sb, q_rows, 6, 2)
         load_blocks(k_sb, k_rows, 4, 4)
         load_blocks(q_sb, q_rows, 4, 2)
 
@@ -75,7 +76,6 @@ def tile_diffattn_pa_kernel(
                 out=x_sb[j][:],
                 in_=x_rows[j * 2 * P : (j + 1) * 2 * P, :].rearrange("(p e) c -> p (e c)", e=2),
             )
-        load_blocks(q_sb, q_rows, 2, 2)
         load_blocks(q_sb, q_rows, 0, 2)
 
         lam_rows = keep.tile([P, P], BF16, name="lam_rows")
@@ -169,16 +169,18 @@ def tile_diffattn_pa_kernel(
             lam_t = psum_t.tile([P, BANK], BF16, tag="tp")
             nc.tensor.transpose(lam_t[:, 0:P], lam_rows[:], ident_bf[:])
             lam_cols = keep.tile([P, 4], F32, name="lam_cols")
-            nc.vector.tensor_copy(out=lam_cols[:], in_=lam_t[:, 0:4])
+            nc.scalar.copy(out=lam_cols[:], in_=lam_t[:, 0:4])
             lam_prod = keep.tile([P, 2], F32, name="lam_prod")
-            nc.vector.tensor_mul(out=lam_prod[:], in0=lam_cols[:, 0:2], in1=lam_cols[:, 2:4])
+            nc.gpsimd.tensor_tensor(
+                out=lam_prod[:], in0=lam_cols[:, 0:2], in1=lam_cols[:, 2:4], op=ALU.mult
+            )
             lam_dot = psum_t.tile([P, BANK], F32, tag="tp")
             nc.tensor.matmul(
                 lam_dot[:, 0:2], lhsT=ones_f32[:], rhs=lam_prod[:], start=True, stop=True
             )
             lam_exp = keep.tile([P, 2], F32, name="lam_exp")
             nc.scalar.activation(out=lam_exp[:], in_=lam_dot[:, 0:2], func=ACT.Exp)
-            nc.vector.tensor_scalar(
+            nc.gpsimd.tensor_scalar(
                 out=neg_lam[:],
                 in0=lam_exp[:, 1:2],
                 scalar1=lam_exp[:, 0:1],
@@ -362,7 +364,7 @@ def tile_diffattn_pa_kernel(
                 )
                 nc.vector.reciprocal(out=inv_sum[:], in_=row_sum[:])
             second = work.tile([P, T], F32, tag="second")
-            nc.vector.tensor_scalar(
+            nc.gpsimd.tensor_scalar(
                 out=second[:, 0:keys],
                 in0=expd[:, T : T + keys],
                 scalar1=inv_sum[:, 1:2],
@@ -418,56 +420,59 @@ def tile_diffattn_pa_kernel(
             nc.scalar.copy(out=o_sb[:], in_=acc[:, 0:H])
             nc.sync.dma_start(out=out_rows[b * P : (b + 1) * P, :], in_=o_sb[:])
 
-        transpose_queries(3)
+        ORDER = [3, 7, 6, 5, 4, 2, 1, 0]
+        PIECES = [(w_sb, w_grouped)] + list(zip(x_sb, x_grouped))
+        PIECES_OF = {1: [0], 2: [1], 3: [2], 4: [3], 5: [4]}
+        transpose_queries(1)
         transpose_keys(0)
+        scores(3, 0)
+        scores(3, 1)
+        transpose_queries(3)
         transpose_keys(1)
-        scores(BLOCKS - 1, 0)
-        scores(BLOCKS - 1, 1)
         finished = []
+        quantised = 0
         for step in range(BLOCKS + 2):
-            cur, mid, old = BLOCKS - 1 - step, BLOCKS - step, BLOCKS + 1 - step
-            if cur >= 0:
+            cur = ORDER[step] if step < BLOCKS else None
+            nxt = ORDER[step + 1] if step + 1 < BLOCKS else None
+            mid = ORDER[step - 1] if 1 <= step <= BLOCKS else None
+            old = ORDER[step - 2] if step >= 2 else None
+            if cur is not None:
                 for h in range(2):
                     row_max(cur, h)
                     exps(cur, h)
-            if 0 <= old < BLOCKS:
+            if old is not None:
                 regroup_att(old)
-            if step == 1:
-                quantise_weight()
-            if step in (2, 3):
-                quantise_x(2 * step - 4)
-                quantise_x(2 * step - 3)
-            if step in (3, 4):
-                quantise_v(step - 3)
-            if 0 <= old < BLOCKS:
+            for i in PIECES_OF.get(step - 1, []):
+                if i == 0:
+                    quantise_weight()
+                else:
+                    quantise_x(i - 1)
+                quantised += 1
+            if step in (5, 7):
+                quantise_v((step - 5) // 2)
+            if old is not None:
                 quantise_att(old)
                 finished.append(old)
-            if 0 <= mid < BLOCKS:
+            if mid is not None:
                 combine(mid)
-            if step == 0:
-                pieces = [(w_sb, w_grouped)]
-            elif step in (1, 2):
-                pieces = [(x_sb[j], x_grouped[j]) for j in (2 * step - 2, 2 * step - 1)]
-            else:
-                pieces = []
-            units = [(src, dst, c_pass) for (src, dst) in pieces for c_pass in range(C_PASSES)]
-            if cur >= 1:
-                scores(cur - 1, 0)
+            units = [(PIECES[i], c_pass) for i in PIECES_OF.get(step, []) for c_pass in range(C_PASSES)]
+            if nxt is not None:
+                scores(nxt, 0)
             if step == 0:
                 compute_lam()
-            if step in (0, 2, 4):
-                transpose_queries(2 - step // 2)
-            for src, dst, c_pass in units[0:2]:
+            if step in (1, 4):
+                transpose_queries({1: 2, 4: 0}[step])
+            for (src, dst), c_pass in units[0:2]:
                 words_onto_partitions(src, dst, c_pass)
-            if cur >= 1:
-                scores(cur - 1, 1)
-            for src, dst, c_pass in units[2:]:
+            if nxt is not None:
+                scores(nxt, 1)
+            for (src, dst), c_pass in units[2:]:
                 words_onto_partitions(src, dst, c_pass)
-            if step in (2, 3):
-                project_v(step - 2)
-            if 0 <= mid < BLOCKS:
+            if step in (4, 6):
+                project_v(step // 2 - 2)
+            if mid is not None:
                 transpose_att(mid)
-            if step >= 4:
+            if step >= 7:
                 for b in finished:
                     attention_output(b)
                 finished = []

@@ -364,7 +364,7 @@ def tile_diffattn_pa_kernel(
                 )
                 nc.vector.reciprocal(out=inv_sum[:], in_=row_sum[:])
             second = work.tile([P, T], F32, tag="second")
-            nc.gpsimd.tensor_scalar(
+            nc.vector.tensor_scalar(
                 out=second[:, 0:keys],
                 in0=expd[:, T : T + keys],
                 scalar1=inv_sum[:, 1:2],

@@ -171,7 +171,7 @@ def tile_diffattn_pa_kernel(
             lam_cols = keep.tile([P, 4], F32, name="lam_cols")
             nc.scalar.copy(out=lam_cols[:], in_=lam_t[:, 0:4])
             lam_prod = keep.tile([P, 2], F32, name="lam_prod")
-            nc.gpsimd.tensor_tensor(
+            nc.vector.tensor_tensor(
                 out=lam_prod[:], in0=lam_cols[:, 0:2], in1=lam_cols[:, 2:4], op=ALU.mult
             )
             lam_dot = psum_t.tile([P, BANK], F32, tag="tp")
@@ -180,7 +180,7 @@ def tile_diffattn_pa_kernel(
             )
             lam_exp = keep.tile([P, 2], F32, name="lam_exp")
             nc.scalar.activation(out=lam_exp[:], in_=lam_dot[:, 0:2], func=ACT.Exp)
-            nc.gpsimd.tensor_scalar(
+            nc.vector.tensor_scalar(
                 out=neg_lam[:],
                 in0=lam_exp[:, 1:2],
                 scalar1=lam_exp[:, 0:1],

@@ -44,11 +44,12 @@ def tile_diffattn_pa_kernel(
 
     with ExitStack() as stack:
         keep = stack.enter_context(tc.tile_pool(name="keep", bufs=1))
-        work = stack.enter_context(tc.tile_pool(name="work", bufs=2))
-        stats = stack.enter_context(tc.tile_pool(name="stats", bufs=3))
+        work = stack.enter_context(tc.tile_pool(name="work", bufs=3))
+        stats = stack.enter_context(tc.tile_pool(name="stats", bufs=5))
         psum_s = stack.enter_context(tc.psum_pool(name="psum_s", bufs=4))
         psum_t = stack.enter_context(tc.psum_pool(name="psum_t", bufs=3))
         psum_a = stack.enter_context(tc.psum_pool(name="psum_a", bufs=1))
+        stack.enter_context(tc.manual_schedule())
 
         k_sb = keep.tile([P, BLOCKS * H], BF16, name="k_sb")
         q_sb = keep.tile([P, BLOCKS * H], BF16, name="q_sb")
@@ -61,9 +62,15 @@ def tile_diffattn_pa_kernel(
 
         load_blocks(q_sb, q_rows, 2, 2)
         load_blocks(k_sb, k_rows, 0, 4)
-        load_blocks(q_sb, q_rows, 6, 2)
+        load_blocks(q_sb, q_rows, 4, 4)
         load_blocks(k_sb, k_rows, 4, 4)
-        load_blocks(q_sb, q_rows, 4, 2)
+
+        lam_rows = keep.tile([P, P], BF16, name="lam_rows")
+        nc.vector.memset(lam_rows[:], 0.0)
+        for r, vec in enumerate((lambda_q1, lambda_q2, lambda_k1, lambda_k2)):
+            nc.sync.dma_start(
+                out=lam_rows[r : r + 1, :], in_=vec.rearrange("(o d) -> o d", o=1)
+            )
 
         w_sb = keep.tile([P, 2 * C], BF16, name="w_sb")
         nc.sync.dma_start(
@@ -77,13 +84,6 @@ def tile_diffattn_pa_kernel(
                 in_=x_rows[j * 2 * P : (j + 1) * 2 * P, :].rearrange("(p e) c -> p (e c)", e=2),
             )
         load_blocks(q_sb, q_rows, 0, 2)
-
-        lam_rows = keep.tile([P, P], BF16, name="lam_rows")
-        nc.vector.memset(lam_rows[:], 0.0)
-        for r, vec in enumerate((lambda_q1, lambda_q2, lambda_k1, lambda_k2)):
-            nc.scalar.dma_start(
-                out=lam_rows[r : r + 1, :], in_=vec.rearrange("(o d) -> o d", o=1)
-            )
 
         ones_f32 = keep.tile([P, P], F32, name="ones_f32")
         nc.vector.memset(ones_f32[:], 1.0)
@@ -131,25 +131,28 @@ def tile_diffattn_pa_kernel(
 
         kT = keep.tile([P, 2 * T], BF16, name="kT")
         qT = keep.tile([P, 2 * T], BF16, name="qT")
+        turned = {}
 
-        def transpose_keys(half):
-            for h in range(2):
-                tp = psum_t.tile([P, BANK], BF16, tag="tp")
-                for i in range(4):
-                    b = half * 4 + i
-                    nc.tensor.transpose(
-                        tp[:, i * P : (i + 1) * P],
-                        k_sb[:, b * H + h * D : b * H + (h + 1) * D],
-                        ident_bf[:],
-                    )
-                dst_cols = kT[:, h * T + half * 512 : h * T + (half + 1) * 512]
-                if h == 0:
-                    nc.vector.tensor_copy(out=dst_cols, in_=tp[:])
-                else:
-                    nc.scalar.copy(out=dst_cols, in_=tp[:])
+        def transpose_keys(half, h):
+            tp = psum_t.tile([P, BANK], BF16, tag="tp")
+            turned[("k", half, h)] = tp
+            for i in range(4):
+                b = half * 4 + i
+                nc.tensor.transpose(
+                    tp[:, i * P : (i + 1) * P],
+                    k_sb[:, b * H + h * D : b * H + (h + 1) * D],
+                    ident_bf[:],
+                )
+
+        def copy_keys(half, h, copy):
+            copy(
+                out=kT[:, h * T + half * 512 : h * T + (half + 1) * 512],
+                in_=turned[("k", half, h)][:],
+            )
 
         def transpose_queries(pair):
             tp = psum_t.tile([P, BANK], BF16, tag="tp")
+            turned[("q", pair)] = tp
             for h in range(2):
                 for i in range(2):
                     b = 2 * pair + i
@@ -158,28 +161,40 @@ def tile_diffattn_pa_kernel(
                         q_sb[:, b * H + h * D : b * H + (h + 1) * D],
                         ident_bf[:],
                     )
-            nc.vector.tensor_copy(
+
+        def copy_queries(pair):
+            nc.scalar.copy(
                 out=qT[:].rearrange("p (h t) -> p h t", h=2)[:, :, 2 * pair * P : (2 * pair + 2) * P],
-                in_=tp[:].rearrange("p (h t) -> p h t", h=2),
+                in_=turned[("q", pair)][:].rearrange("p (h t) -> p h t", h=2),
             )
 
         neg_lam = keep.tile([P, 1], F32, name="neg_lam")
+        lam_cols = keep.tile([P, 4], F32, name="lam_cols")
+        lam_prod = keep.tile([P, 2], F32, name="lam_prod")
+        lam_exp = keep.tile([P, 2], F32, name="lam_exp")
 
-        def compute_lam():
-            lam_t = psum_t.tile([P, BANK], BF16, tag="tp")
+        def lam_transpose():
+            lam_t = psum_a.tile([P, BANK], BF16, tag="at")
+            turned["lam"] = lam_t
             nc.tensor.transpose(lam_t[:, 0:P], lam_rows[:], ident_bf[:])
-            lam_cols = keep.tile([P, 4], F32, name="lam_cols")
-            nc.scalar.copy(out=lam_cols[:], in_=lam_t[:, 0:4])
-            lam_prod = keep.tile([P, 2], F32, name="lam_prod")
-            nc.vector.tensor_tensor(
-                out=lam_prod[:], in0=lam_cols[:, 0:2], in1=lam_cols[:, 2:4], op=ALU.mult
-            )
-            lam_dot = psum_t.tile([P, BANK], F32, tag="tp")
+
+        def lam_columns():
+            nc.scalar.copy(out=lam_cols[:], in_=turned["lam"][:, 0:4])
+
+        def lam_products():
+            nc.vector.tensor_mul(out=lam_prod[:], in0=lam_cols[:, 0:2], in1=lam_cols[:, 2:4])
+
+        def lam_sums():
+            lam_dot = psum_a.tile([P, BANK], F32, tag="at")
+            turned["dot"] = lam_dot
             nc.tensor.matmul(
                 lam_dot[:, 0:2], lhsT=ones_f32[:], rhs=lam_prod[:], start=True, stop=True
             )
-            lam_exp = keep.tile([P, 2], F32, name="lam_exp")
-            nc.scalar.activation(out=lam_exp[:], in_=lam_dot[:, 0:2], func=ACT.Exp)
+
+        def lam_exps():
+            nc.scalar.activation(out=lam_exp[:], in_=turned["dot"][:, 0:2], func=ACT.Exp)
+
+        def lam_negative():
             nc.vector.tensor_scalar(
                 out=neg_lam[:],
                 in0=lam_exp[:, 1:2],
@@ -188,27 +203,6 @@ def tile_diffattn_pa_kernel(
                 op0=ALU.subtract,
                 op1=ALU.subtract,
             )
-
-        def words_onto_partitions(src, grouped, c_pass):
-            src_words = src[:].bitcast(F32)
-            tp = psum_t.tile([P, BANK], F32, tag="tp")
-            for u in range(2):
-                for a in range(2):
-                    first = a * (C // 2) + (2 * c_pass + u) * P
-                    nc.tensor.transpose(
-                        tp[:, (u * 2 + a) * P : (u * 2 + a + 1) * P],
-                        src_words[:, first : first + P],
-                        ident_f32[:],
-                    )
-            dst = (
-                grouped[:]
-                .bitcast(F32)[:, c_pass * BANK : (c_pass + 1) * BANK]
-                .rearrange("p (n u) -> p n u", u=2)
-            )
-            if c_pass == C_PASSES - 1:
-                nc.vector.tensor_copy(out=dst, in_=tp[:].rearrange("p (u n) -> p n u", u=2))
-            else:
-                nc.scalar.copy(out=dst, in_=tp[:].rearrange("p (u n) -> p n u", u=2))
 
         GROUP_WORDS = C_PASSES * 2 * P
         w_grouped = keep.tile([P, GROUP_WORDS * 4], BF16, name="w_grouped", align_bytes=64)
@@ -220,43 +214,70 @@ def tile_diffattn_pa_kernel(
         ]
         x_codes = keep.tile([P, PAIRS * GROUP_WORDS], U32, name="x_codes", align_bytes=64)
         x_scales = keep.tile([P, PAIRS * GROUP_WORDS], U8, name="x_scales", align_bytes=64)
+        piece_rows = [w_sb] + x_sb
+        piece_grouped = [w_grouped] + x_grouped
 
-        def quantise_weight():
-            nc.vector.quantize_mx(
-                out=w_codes[:].bitcast(FP8X4), scales=w_scales[:], in_=w_grouped[:]
+        def words_onto_partitions(i, c_pass):
+            src_words = piece_rows[i][:].bitcast(F32)
+            tp = psum_t.tile([P, BANK], F32, tag="tp")
+            turned[(i, c_pass)] = tp
+            for u in range(2):
+                for a in range(2):
+                    first = a * (C // 2) + (2 * c_pass + u) * P
+                    nc.tensor.transpose(
+                        tp[:, (u * 2 + a) * P : (u * 2 + a + 1) * P],
+                        src_words[:, first : first + P],
+                        ident_f32[:],
+                    )
+
+        def regroup_words(i, c_pass, copy):
+            copy(
+                out=piece_grouped[i][:]
+                .bitcast(F32)[:, c_pass * BANK : (c_pass + 1) * BANK]
+                .rearrange("p (n u) -> p n u", u=2),
+                in_=turned[(i, c_pass)][:].rearrange("p (u n) -> p n u", u=2),
             )
 
-        def quantise_x(j):
-            cols = slice(j * GROUP_WORDS, (j + 1) * GROUP_WORDS)
-            nc.vector.quantize_mx(
-                out=x_codes[:, cols].bitcast(FP8X4), scales=x_scales[:, cols], in_=x_grouped[j][:]
-            )
+        def quantise_piece(i):
+            if i == 0:
+                nc.vector.quantize_mx(
+                    out=w_codes[:].bitcast(FP8X4), scales=w_scales[:], in_=w_grouped[:]
+                )
+            else:
+                cols = slice((i - 1) * GROUP_WORDS, i * GROUP_WORDS)
+                nc.vector.quantize_mx(
+                    out=x_codes[:, cols].bitcast(FP8X4),
+                    scales=x_scales[:, cols],
+                    in_=x_grouped[i - 1][:],
+                )
 
         v_grouped = keep.tile([P, KEY_PASSES * H * 4], BF16, name="v_grouped", align_bytes=64)
         v_codes = keep.tile([P, KEY_PASSES * H], U32, name="v_codes", align_bytes=64)
         v_scales = keep.tile([P, KEY_PASSES * H], U8, name="v_scales", align_bytes=64)
 
-        def project_v(g):
-            for half in range(2):
-                acc = psum_t.tile([P, BANK], F32, tag="tp")
-                for t in range(4):
-                    for c_pass in range(C_PASSES):
-                        x_first = ((2 * g + t // 2) * C_PASSES + c_pass) * 2 * P + (t % 2) * P
-                        w_first = c_pass * H + half * P
-                        nc.tensor.matmul_mx(
-                            out=acc[:, t * P : (t + 1) * P],
-                            lhsT=x_codes[:, x_first : x_first + P].bitcast(FP8X4),
-                            lhsT_scale=x_scales[:, x_first : x_first + P],
-                            rhs=w_codes[:, w_first : w_first + P].bitcast(FP8X4),
-                            rhs_scale=w_scales[:, w_first : w_first + P],
-                            start=(c_pass == 0),
-                            stop=(c_pass == C_PASSES - 1),
-                        )
-                first = (g * 2 + half) * BANK
-                nc.scalar.copy(
-                    out=v_grouped[:, first : first + BANK].rearrange("p (n t) -> p n t", t=4),
-                    in_=acc[:].rearrange("p (t n) -> p n t", t=4),
-                )
+        def project_v(g, half, pool, tag):
+            acc = pool.tile([P, BANK], F32, tag=tag)
+            turned[("v", g, half)] = acc
+            for t in range(4):
+                for c_pass in range(C_PASSES):
+                    x_first = ((2 * g + t // 2) * C_PASSES + c_pass) * 2 * P + (t % 2) * P
+                    w_first = c_pass * H + half * P
+                    nc.tensor.matmul_mx(
+                        out=acc[:, t * P : (t + 1) * P],
+                        lhsT=x_codes[:, x_first : x_first + P].bitcast(FP8X4),
+                        lhsT_scale=x_scales[:, x_first : x_first + P],
+                        rhs=w_codes[:, w_first : w_first + P].bitcast(FP8X4),
+                        rhs_scale=w_scales[:, w_first : w_first + P],
+                        start=(c_pass == 0),
+                        stop=(c_pass == C_PASSES - 1),
+                    )
+
+        def regroup_v(g, half):
+            first = (g * 2 + half) * BANK
+            nc.scalar.copy(
+                out=v_grouped[:, first : first + BANK].rearrange("p (n t) -> p n t", t=4),
+                in_=turned[("v", g, half)][:].rearrange("p (t n) -> p n t", t=4),
+            )
 
         def quantise_v(g):
             nc.vector.quantize_mx(
@@ -268,6 +289,9 @@ def tile_diffattn_pa_kernel(
         score_banks = {}
         stat_tiles = {}
         exp_tiles = {}
+        inv_sums = {}
+        row_sum_tiles = {}
+        seconds = {}
 
         def scores(b, h):
             keys = (b + 1) * P
@@ -300,20 +324,23 @@ def tile_diffattn_pa_kernel(
                         stop=True,
                     )
 
-        def row_max(b, h):
-            if h == 0:
+        def bank_maximum(b, h, c):
+            if b not in stat_tiles:
                 bank_max = stats.tile([P, 4], F32, tag="bank_max")
                 neg_max = stats.tile([P, 2], F32, tag="neg_max")
                 bank_sum = stats.tile([P, 4], F32, tag="bank_sum")
                 stat_tiles[b] = (bank_max, neg_max, bank_sum)
             bank_max, neg_max, bank_sum = stat_tiles[b]
-            for c, (sc, first, width) in enumerate(score_banks[(b, h)]):
-                nc.vector.tensor_reduce(
-                    out=bank_max[:, 2 * h + c : 2 * h + c + 1],
-                    in_=sc[:, 0:width],
-                    axis=AXIS_X,
-                    op=ALU.max,
-                )
+            sc, first, width = score_banks[(b, h)][c]
+            nc.vector.tensor_reduce(
+                out=bank_max[:, 2 * h + c : 2 * h + c + 1],
+                in_=sc[:, 0:width],
+                axis=AXIS_X,
+                op=ALU.max,
+            )
+
+        def negative_maximum(b, h):
+            bank_max, neg_max, bank_sum = stat_tiles[b]
             if key_passes_of[b] == 1:
                 nc.vector.tensor_scalar(
                     out=neg_max[:, h : h + 1],
@@ -333,7 +360,7 @@ def tile_diffattn_pa_kernel(
                 )
 
         def exps(b, h):
-            if h == 0:
+            if b not in exp_tiles:
                 expd = work.tile([P, 2 * T], F32, tag="expd")
                 exp_tiles[b] = expd
             bank_max, neg_max, bank_sum = stat_tiles[b]
@@ -347,46 +374,54 @@ def tile_diffattn_pa_kernel(
                     accum_out=bank_sum[:, 2 * h + c : 2 * h + c + 1],
                 )
 
-        def combine(b):
-            keys = (b + 1) * P
+        def row_sums(b):
             bank_max, neg_max, bank_sum = stat_tiles[b]
-            expd = exp_tiles[b]
+            row_sum = stats.tile([P, 2], F32, tag="row_sum")
+            row_sum_tiles[b] = row_sum
+            nc.vector.tensor_reduce(
+                out=row_sum[:],
+                in_=bank_sum[:].rearrange("p (h c) -> p h c", c=2),
+                axis=AXIS_X,
+                op=ALU.add,
+            )
+
+        def inverse_sums(b):
+            bank_max, neg_max, bank_sum = stat_tiles[b]
             inv_sum = stats.tile([P, 2], F32, tag="inv_sum")
+            inv_sums[b] = inv_sum
             if key_passes_of[b] == 1:
                 nc.vector.reciprocal(out=inv_sum[:], in_=bank_sum[:, 0:4:2])
             else:
-                row_sum = stats.tile([P, 2], F32, tag="row_sum")
-                nc.vector.tensor_reduce(
-                    out=row_sum[:],
-                    in_=bank_sum[:].rearrange("p (h c) -> p h c", c=2),
-                    axis=AXIS_X,
-                    op=ALU.add,
-                )
-                nc.vector.reciprocal(out=inv_sum[:], in_=row_sum[:])
+                nc.vector.reciprocal(out=inv_sum[:], in_=row_sum_tiles[b][:])
+
+        def scale_second(b):
+            keys = (b + 1) * P
             second = work.tile([P, T], F32, tag="second")
+            seconds[b] = second
             nc.vector.tensor_scalar(
                 out=second[:, 0:keys],
-                in0=expd[:, T : T + keys],
-                scalar1=inv_sum[:, 1:2],
+                in0=exp_tiles[b][:, T : T + keys],
+                scalar1=inv_sums[b][:, 1:2],
                 scalar2=neg_lam[:, 0:1],
                 op0=ALU.mult,
                 op1=ALU.mult,
             )
+
+        def combine(b):
+            keys = (b + 1) * P
             nc.vector.scalar_tensor_tensor(
                 out=att[b][:, 0:keys],
-                in0=expd[:, 0:keys],
-                scalar=inv_sum[:, 0:1],
-                in1=second[:, 0:keys],
+                in0=exp_tiles[b][:, 0:keys],
+                scalar=inv_sums[b][:, 0:1],
+                in1=seconds[b][:, 0:keys],
                 op0=ALU.mult,
                 op1=ALU.add,
             )
 
-        att_banks = {}
-
         def transpose_att(b):
             att_words = att[b][:].bitcast(F32)
             at = psum_a.tile([P, BANK], F32, tag="at")
-            att_banks[b] = at
+            turned[("att", b)] = at
             for i in range(key_passes_of[b] * 2):
                 nc.tensor.transpose(
                     at[:, i * P : (i + 1) * P], att_words[:, i * P : (i + 1) * P], ident_f32[:]
@@ -396,7 +431,7 @@ def tile_diffattn_pa_kernel(
             g = key_passes_of[b]
             nc.scalar.copy(
                 out=att_grouped[b][:].bitcast(F32).rearrange("p (g n u) -> p g n u", g=g, u=2),
-                in_=att_banks[b][:, 0 : g * 2 * P].rearrange("p (g u n) -> p g n u", g=g, u=2),
+                in_=turned[("att", b)][:, 0 : g * 2 * P].rearrange("p (g u n) -> p g n u", g=g, u=2),
             )
 
         def quantise_att(b):
@@ -404,8 +439,9 @@ def tile_diffattn_pa_kernel(
                 out=att_codes[b][:].bitcast(FP8X4), scales=att_scales[b][:], in_=att_grouped[b][:]
             )
 
-        def attention_output(b):
-            acc = psum_t.tile([P, BANK], F32, tag="tp")
+        def attention_output(b, pool, tag):
+            acc = pool.tile([P, BANK], F32, tag=tag)
+            turned[("out", b)] = acc
             for g in range(key_passes_of[b]):
                 nc.tensor.matmul_mx(
                     out=acc[:, 0:H],
@@ -416,63 +452,226 @@ def tile_diffattn_pa_kernel(
                     start=(g == 0),
                     stop=(g == key_passes_of[b] - 1),
                 )
+
+        def store_output(b, copy):
             o_sb = keep.tile([P, H], F32, name="o_sb%d" % b)
-            nc.scalar.copy(out=o_sb[:], in_=acc[:, 0:H])
+            copy(out=o_sb[:], in_=turned[("out", b)][:, 0:H])
             nc.sync.dma_start(out=out_rows[b * P : (b + 1) * P, :], in_=o_sb[:])
 
-        ORDER = [3, 7, 6, 5, 4, 2, 1, 0]
-        PIECES = [(w_sb, w_grouped)] + list(zip(x_sb, x_grouped))
-        PIECES_OF = {1: [0], 2: [1], 3: [2], 4: [3], 5: [4]}
         transpose_queries(1)
-        transpose_keys(0)
+        transpose_keys(0, 0)
+        transpose_keys(0, 1)
+        copy_keys(0, 0, nc.vector.tensor_copy)
+        copy_keys(0, 1, nc.vector.tensor_copy)
+        copy_queries(1)
+        transpose_queries(3)
+        transpose_keys(1, 0)
         scores(3, 0)
         scores(3, 1)
-        transpose_queries(3)
-        transpose_keys(1)
-        finished = []
-        quantised = 0
-        for step in range(BLOCKS + 2):
-            cur = ORDER[step] if step < BLOCKS else None
-            nxt = ORDER[step + 1] if step + 1 < BLOCKS else None
-            mid = ORDER[step - 1] if 1 <= step <= BLOCKS else None
-            old = ORDER[step - 2] if step >= 2 else None
-            if cur is not None:
-                for h in range(2):
-                    row_max(cur, h)
-                    exps(cur, h)
-            if old is not None:
-                regroup_att(old)
-            for i in PIECES_OF.get(step - 1, []):
-                if i == 0:
-                    quantise_weight()
-                else:
-                    quantise_x(i - 1)
-                quantised += 1
-            if step in (5, 7):
-                quantise_v((step - 5) // 2)
-            if old is not None:
-                quantise_att(old)
-                finished.append(old)
-            if mid is not None:
-                combine(mid)
-            units = [(PIECES[i], c_pass) for i in PIECES_OF.get(step, []) for c_pass in range(C_PASSES)]
-            if nxt is not None:
-                scores(nxt, 0)
-            if step == 0:
-                compute_lam()
-            if step in (1, 4):
-                transpose_queries({1: 2, 4: 0}[step])
-            for (src, dst), c_pass in units[0:2]:
-                words_onto_partitions(src, dst, c_pass)
-            if nxt is not None:
-                scores(nxt, 1)
-            for (src, dst), c_pass in units[2:]:
-                words_onto_partitions(src, dst, c_pass)
-            if step in (4, 6):
-                project_v(step // 2 - 2)
-            if mid is not None:
-                transpose_att(mid)
-            if step >= 7:
-                for b in finished:
-                    attention_output(b)
-                finished = []
+        lam_transpose()
+        transpose_keys(1, 1)
+        copy_keys(1, 0, nc.vector.tensor_copy)
+        bank_maximum(3, 0, 0)
+        negative_maximum(3, 0)
+        bank_maximum(3, 1, 0)
+        copy_queries(3)
+        copy_keys(1, 1, nc.scalar.copy)
+        lam_columns()
+        exps(3, 0)
+        scores(7, 0)
+        lam_products()
+        negative_maximum(3, 1)
+        bank_maximum(7, 0, 0)
+        bank_maximum(7, 0, 1)
+        lam_sums()
+        lam_exps()
+        exps(3, 1)
+        scores(7, 1)
+        words_onto_partitions(0, 0)
+        words_onto_partitions(0, 1)
+        words_onto_partitions(0, 2)
+        lam_negative()
+        negative_maximum(7, 0)
+        inverse_sums(3)
+        scale_second(3)
+        bank_maximum(7, 1, 0)
+        bank_maximum(7, 1, 1)
+        negative_maximum(7, 1)
+        combine(3)
+        regroup_words(0, 2, nc.vector.tensor_copy)
+        exps(7, 0)
+        regroup_words(0, 0, nc.scalar.copy)
+        regroup_words(0, 1, nc.scalar.copy)
+        exps(7, 1)
+        scores(6, 0)
+        words_onto_partitions(0, 3)
+        words_onto_partitions(1, 0)
+        transpose_att(3)
+        scores(6, 1)
+        words_onto_partitions(1, 1)
+        regroup_words(0, 3, nc.vector.tensor_copy)
+        bank_maximum(6, 0, 0)
+        bank_maximum(6, 0, 1)
+        row_sums(7)
+        negative_maximum(6, 0)
+        inverse_sums(7)
+        bank_maximum(6, 1, 0)
+        scale_second(7)
+        bank_maximum(6, 1, 1)
+        regroup_words(1, 0, nc.scalar.copy)
+        regroup_att(3)
+        transpose_queries(2)
+        words_onto_partitions(1, 2)
+        quantise_att(3)
+        negative_maximum(6, 1)
+        combine(7)
+        quantise_piece(0)
+        copy_queries(2)
+        exps(6, 0)
+        regroup_words(1, 1, nc.scalar.copy)
+        regroup_words(1, 2, nc.scalar.copy)
+        exps(6, 1)
+        scores(5, 0)
+        words_onto_partitions(1, 3)
+        words_onto_partitions(2, 0)
+        words_onto_partitions(2, 1)
+        transpose_att(7)
+        scores(5, 1)
+        bank_maximum(5, 0, 0)
+        bank_maximum(5, 0, 1)
+        row_sums(6)
+        negative_maximum(5, 0)
+        inverse_sums(6)
+        bank_maximum(5, 1, 0)
+        scale_second(6)
+        bank_maximum(5, 1, 1)
+        regroup_words(1, 3, nc.scalar.copy)
+        regroup_words(2, 0, nc.scalar.copy)
+        regroup_att(7)
+        exps(5, 0)
+        regroup_words(2, 1, nc.scalar.copy)
+        words_onto_partitions(2, 2)
+        words_onto_partitions(2, 3)
+        scores(4, 0)
+        words_onto_partitions(3, 0)
+        quantise_att(7)
+        negative_maximum(5, 1)
+        combine(6)
+        quantise_piece(1)
+        bank_maximum(4, 0, 0)
+        bank_maximum(4, 0, 1)
+        regroup_words(2, 2, nc.scalar.copy)
+        exps(5, 1)
+        regroup_words(2, 3, nc.scalar.copy)
+        regroup_words(3, 0, nc.scalar.copy)
+        words_onto_partitions(3, 1)
+        transpose_att(6)
+        scores(4, 1)
+        words_onto_partitions(3, 2)
+        transpose_queries(0)
+        row_sums(5)
+        negative_maximum(4, 0)
+        inverse_sums(5)
+        bank_maximum(4, 1, 0)
+        scale_second(5)
+        bank_maximum(4, 1, 1)
+        regroup_att(6)
+        exps(4, 0)
+        regroup_words(3, 1, nc.scalar.copy)
+        regroup_words(3, 2, nc.scalar.copy)
+        scores(2, 0)
+        words_onto_partitions(3, 3)
+        words_onto_partitions(4, 0)
+        quantise_att(6)
+        negative_maximum(4, 1)
+        combine(5)
+        quantise_piece(2)
+        bank_maximum(2, 0, 0)
+        exps(4, 1)
+        copy_queries(0)
+        regroup_words(3, 3, nc.scalar.copy)
+        regroup_words(4, 0, nc.scalar.copy)
+        transpose_att(5)
+        scores(2, 1)
+        words_onto_partitions(4, 1)
+        words_onto_partitions(4, 2)
+        words_onto_partitions(4, 3)
+        project_v(0, 0, psum_s, "sc")
+        project_v(0, 1, psum_s, "sc")
+        row_sums(4)
+        negative_maximum(2, 0)
+        bank_maximum(2, 1, 0)
+        inverse_sums(4)
+        negative_maximum(2, 1)
+        quantise_piece(3)
+        scale_second(4)
+        regroup_att(5)
+        regroup_words(4, 1, nc.scalar.copy)
+        regroup_words(4, 2, nc.scalar.copy)
+        regroup_words(4, 3, nc.scalar.copy)
+        regroup_v(0, 0)
+        exps(2, 0)
+        exps(2, 1)
+        regroup_v(0, 1)
+        scores(1, 0)
+        scores(1, 1)
+        quantise_piece(4)
+        combine(4)
+        bank_maximum(1, 0, 0)
+        bank_maximum(1, 1, 0)
+        negative_maximum(1, 0)
+        inverse_sums(2)
+        negative_maximum(1, 1)
+        scale_second(2)
+        quantise_att(5)
+        combine(2)
+        exps(1, 0)
+        transpose_att(4)
+        project_v(1, 0, psum_t, "tp")
+        scores(0, 0)
+        scores(0, 1)
+        bank_maximum(0, 0, 0)
+        bank_maximum(0, 1, 0)
+        negative_maximum(0, 0)
+        quantise_v(0)
+        negative_maximum(0, 1)
+        regroup_att(4)
+        exps(1, 1)
+        exps(0, 0)
+        exps(0, 1)
+        regroup_v(1, 0)
+        transpose_att(2)
+        project_v(1, 1, psum_t, "tp")
+        inverse_sums(1)
+        scale_second(1)
+        quantise_att(4)
+        combine(1)
+        inverse_sums(0)
+        scale_second(0)
+        regroup_att(2)
+        regroup_v(1, 1)
+        transpose_att(1)
+        attention_output(3, psum_t, "tp")
+        quantise_att(2)
+        combine(0)
+        quantise_v(1)
+        store_output(3, nc.vector.tensor_copy)
+        regroup_att(1)
+        transpose_att(0)
+        attention_output(7, psum_s, "sc")
+        attention_output(6, psum_s, "sc")
+        attention_output(5, psum_s, "sc")
+        quantise_att(1)
+        store_output(6, nc.vector.tensor_copy)
+        regroup_att(0)
+        store_output(7, nc.scalar.copy)
+        store_output(5, nc.scalar.copy)
+        attention_output(4, psum_s, "sc")
+        attention_output(2, psum_s, "sc")
+        attention_output(1, psum_s, "sc")
+        quantise_att(0)
+        store_output(4, nc.vector.tensor_copy)
+        store_output(1, nc.vector.tensor_copy)
+        store_output(2, nc.scalar.copy)
+        attention_output(0, psum_s, "sc")
+        store_output(0, nc.scalar.copy)

@@ -47,8 +47,7 @@ def tile_diffattn_pa_kernel(
         work = stack.enter_context(tc.tile_pool(name="work", bufs=3))
         stats = stack.enter_context(tc.tile_pool(name="stats", bufs=5))
         psum_s = stack.enter_context(tc.psum_pool(name="psum_s", bufs=4))
-        psum_t = stack.enter_context(tc.psum_pool(name="psum_t", bufs=3))
-        psum_a = stack.enter_context(tc.psum_pool(name="psum_a", bufs=1))
+        psum_t = stack.enter_context(tc.psum_pool(name="psum_t", bufs=4))
         stack.enter_context(tc.manual_schedule())
 
         k_sb = keep.tile([P, BLOCKS * H], BF16, name="k_sb")
@@ -174,7 +173,7 @@ def tile_diffattn_pa_kernel(
         lam_exp = keep.tile([P, 2], F32, name="lam_exp")
 
         def lam_transpose():
-            lam_t = psum_a.tile([P, BANK], BF16, tag="at")
+            lam_t = psum_t.tile([P, BANK], BF16, tag="tp")
             turned["lam"] = lam_t
             nc.tensor.transpose(lam_t[:, 0:P], lam_rows[:], ident_bf[:])
 
@@ -185,7 +184,7 @@ def tile_diffattn_pa_kernel(
             nc.vector.tensor_mul(out=lam_prod[:], in0=lam_cols[:, 0:2], in1=lam_cols[:, 2:4])
 
         def lam_sums():
-            lam_dot = psum_a.tile([P, BANK], F32, tag="at")
+            lam_dot = psum_t.tile([P, BANK], F32, tag="tp")
             turned["dot"] = lam_dot
             nc.tensor.matmul(
                 lam_dot[:, 0:2], lhsT=ones_f32[:], rhs=lam_prod[:], start=True, stop=True
@@ -298,20 +297,12 @@ def tile_diffattn_pa_kernel(
             banks = key_passes_of[b]
             queries = qT[:, h * T + b * P : h * T + (b + 1) * P]
             score_banks[(b, h)] = []
-            for c in range(banks):
+            for c in reversed(range(banks)):
                 first = c * BANK
                 width = min(keys - first, BANK)
                 sc = psum_s.tile([P, BANK], F32, tag="sc")
                 score_banks[(b, h)].append((sc, first, width))
                 before = width - P if c == banks - 1 else width
-                if before > 0:
-                    nc.tensor.matmul(
-                        sc[:, 0:before],
-                        lhsT=queries,
-                        rhs=kT[:, h * T + first : h * T + first + before],
-                        start=True,
-                        stop=True,
-                    )
                 if c == banks - 1:
                     nc.tensor.matmul(
                         sc[:, before:width], lhsT=ident_bf[:], rhs=mask_bf[:], start=True, stop=False
@@ -321,6 +312,14 @@ def tile_diffattn_pa_kernel(
                         lhsT=queries,
                         rhs=kT[:, h * T + first + before : h * T + first + width],
                         start=False,
+                        stop=True,
+                    )
+                if before > 0:
+                    nc.tensor.matmul(
+                        sc[:, 0:before],
+                        lhsT=queries,
+                        rhs=kT[:, h * T + first : h * T + first + before],
+                        start=True,
                         stop=True,
                     )
 
@@ -420,7 +419,7 @@ def tile_diffattn_pa_kernel(
 
         def transpose_att(b):
             att_words = att[b][:].bitcast(F32)
-            at = psum_a.tile([P, BANK], F32, tag="at")
+            at = psum_t.tile([P, BANK], F32, tag="tp")
             turned[("att", b)] = at
             for i in range(key_passes_of[b] * 2):
                 nc.tensor.transpose(
@@ -461,10 +460,11 @@ def tile_diffattn_pa_kernel(
         transpose_queries(1)
         transpose_keys(0, 0)
         transpose_keys(0, 1)
+        transpose_queries(3)
         copy_keys(0, 0, nc.vector.tensor_copy)
         copy_keys(0, 1, nc.vector.tensor_copy)
         copy_queries(1)
-        transpose_queries(3)
+        copy_queries(3)
         transpose_keys(1, 0)
         scores(3, 0)
         scores(3, 1)
@@ -474,7 +474,6 @@ def tile_diffattn_pa_kernel(
         bank_maximum(3, 0, 0)
         negative_maximum(3, 0)
         bank_maximum(3, 1, 0)
-        copy_queries(3)
         copy_keys(1, 1, nc.scalar.copy)
         lam_columns()
         exps(3, 0)
@@ -490,6 +489,7 @@ def tile_diffattn_pa_kernel(
         words_onto_partitions(0, 0)
         words_onto_partitions(0, 1)
         words_onto_partitions(0, 2)
+        words_onto_partitions(0, 3)
         lam_negative()
         negative_maximum(7, 0)
         inverse_sums(3)
@@ -499,17 +499,17 @@ def tile_diffattn_pa_kernel(
         negative_maximum(7, 1)
         combine(3)
         regroup_words(0, 2, nc.vector.tensor_copy)
+        regroup_words(0, 3, nc.vector.tensor_copy)
         exps(7, 0)
         regroup_words(0, 0, nc.scalar.copy)
         regroup_words(0, 1, nc.scalar.copy)
         exps(7, 1)
         scores(6, 0)
-        words_onto_partitions(0, 3)
         words_onto_partitions(1, 0)
         transpose_att(3)
         scores(6, 1)
+        transpose_queries(2)
         words_onto_partitions(1, 1)
-        regroup_words(0, 3, nc.vector.tensor_copy)
         bank_maximum(6, 0, 0)
         bank_maximum(6, 0, 1)
         row_sums(7)
@@ -520,52 +520,51 @@ def tile_diffattn_pa_kernel(
         bank_maximum(6, 1, 1)
         regroup_words(1, 0, nc.scalar.copy)
         regroup_att(3)
-        transpose_queries(2)
+        copy_queries(2)
+        exps(6, 0)
+        regroup_words(1, 1, nc.scalar.copy)
         words_onto_partitions(1, 2)
+        words_onto_partitions(1, 3)
+        scores(5, 0)
+        words_onto_partitions(2, 0)
         quantise_att(3)
         negative_maximum(6, 1)
         combine(7)
         quantise_piece(0)
-        copy_queries(2)
-        exps(6, 0)
-        regroup_words(1, 1, nc.scalar.copy)
-        regroup_words(1, 2, nc.scalar.copy)
-        exps(6, 1)
-        scores(5, 0)
-        words_onto_partitions(1, 3)
-        words_onto_partitions(2, 0)
-        words_onto_partitions(2, 1)
-        transpose_att(7)
-        scores(5, 1)
         bank_maximum(5, 0, 0)
         bank_maximum(5, 0, 1)
+        regroup_words(1, 2, nc.scalar.copy)
+        exps(6, 1)
+        regroup_words(1, 3, nc.scalar.copy)
+        regroup_words(2, 0, nc.scalar.copy)
+        transpose_att(7)
+        scores(5, 1)
+        words_onto_partitions(2, 1)
+        words_onto_partitions(2, 2)
+        words_onto_partitions(2, 3)
         row_sums(6)
         negative_maximum(5, 0)
         inverse_sums(6)
         bank_maximum(5, 1, 0)
         scale_second(6)
         bank_maximum(5, 1, 1)
-        regroup_words(1, 3, nc.scalar.copy)
-        regroup_words(2, 0, nc.scalar.copy)
         regroup_att(7)
         exps(5, 0)
         regroup_words(2, 1, nc.scalar.copy)
-        words_onto_partitions(2, 2)
-        words_onto_partitions(2, 3)
-        scores(4, 0)
+        regroup_words(2, 2, nc.scalar.copy)
         words_onto_partitions(3, 0)
+        scores(4, 0)
         quantise_att(7)
         negative_maximum(5, 1)
         combine(6)
         quantise_piece(1)
         bank_maximum(4, 0, 0)
         bank_maximum(4, 0, 1)
-        regroup_words(2, 2, nc.scalar.copy)
         exps(5, 1)
         regroup_words(2, 3, nc.scalar.copy)
         regroup_words(3, 0, nc.scalar.copy)
-        words_onto_partitions(3, 1)
         transpose_att(6)
+        words_onto_partitions(3, 1)
         scores(4, 1)
         words_onto_partitions(3, 2)
         transpose_queries(0)
@@ -579,8 +578,8 @@ def tile_diffattn_pa_kernel(
         exps(4, 0)
         regroup_words(3, 1, nc.scalar.copy)
         regroup_words(3, 2, nc.scalar.copy)
-        scores(2, 0)
         words_onto_partitions(3, 3)
+        scores(2, 0)
         words_onto_partitions(4, 0)
         quantise_att(6)
         negative_maximum(4, 1)
@@ -605,6 +604,7 @@ def tile_diffattn_pa_kernel(
         negative_maximum(2, 1)
         quantise_piece(3)
         scale_second(4)
+        combine(4)
         regroup_att(5)
         regroup_words(4, 1, nc.scalar.copy)
         regroup_words(4, 2, nc.scalar.copy)
@@ -615,8 +615,8 @@ def tile_diffattn_pa_kernel(
         regroup_v(0, 1)
         scores(1, 0)
         scores(1, 1)
+        transpose_att(4)
         quantise_piece(4)
-        combine(4)
         bank_maximum(1, 0, 0)
         bank_maximum(1, 1, 0)
         negative_maximum(1, 0)
@@ -626,32 +626,31 @@ def tile_diffattn_pa_kernel(
         quantise_att(5)
         combine(2)
         exps(1, 0)
-        transpose_att(4)
+        regroup_att(4)
+        exps(1, 1)
         project_v(1, 0, psum_t, "tp")
         scores(0, 0)
         scores(0, 1)
+        transpose_att(2)
+        project_v(1, 1, psum_t, "tp")
         bank_maximum(0, 0, 0)
         bank_maximum(0, 1, 0)
         negative_maximum(0, 0)
         quantise_v(0)
         negative_maximum(0, 1)
-        regroup_att(4)
-        exps(1, 1)
-        exps(0, 0)
-        exps(0, 1)
-        regroup_v(1, 0)
-        transpose_att(2)
-        project_v(1, 1, psum_t, "tp")
         inverse_sums(1)
         scale_second(1)
         quantise_att(4)
         combine(1)
-        inverse_sums(0)
-        scale_second(0)
+        exps(0, 0)
+        exps(0, 1)
+        regroup_v(1, 0)
         regroup_att(2)
         regroup_v(1, 1)
         transpose_att(1)
         attention_output(3, psum_t, "tp")
+        inverse_sums(0)
+        scale_second(0)
         quantise_att(2)
         combine(0)
         quantise_v(1)

@@ -220,6 +220,10 @@ def tile_diffattn_pa_kernel(
             src_words = piece_rows[i][:].bitcast(F32)
             tp = psum_t.tile([P, BANK], F32, tag="tp")
             turned[(i, c_pass)] = tp
+            if i > 0:
+                nc.tensor.matmul(
+                    tp[:, 0:256], lhsT=ident_bf[:], rhs=k_sb[:, 0:256], start=True, stop=True
+                )
             for u in range(2):
                 for a in range(2):
                     first = a * (C // 2) + (2 * c_pass + u) * P

@@ -50,6 +50,9 @@ def tile_diffattn_pa_kernel(
         psum_t = stack.enter_context(tc.psum_pool(name="psum_t", bufs=4))
         stack.enter_context(tc.manual_schedule())
 
+        warm_bf = keep.tile([P, 2 * P], BF16, name="warm_bf")
+        nc.vector.memset(warm_bf[:], 0.0)
+
         k_sb = keep.tile([P, BLOCKS * H], BF16, name="k_sb")
         q_sb = keep.tile([P, BLOCKS * H], BF16, name="q_sb")
 
@@ -220,9 +223,19 @@ def tile_diffattn_pa_kernel(
             src_words = piece_rows[i][:].bitcast(F32)
             tp = psum_t.tile([P, BANK], F32, tag="tp")
             turned[(i, c_pass)] = tp
-            if i > 0:
+            if i > 2 and c_pass % 2 == 0:
+                nc.tensor.matmul_mx(
+                    out=tp[:],
+                    lhsT=w_codes[:, 0:P].bitcast(FP8X4),
+                    lhsT_scale=w_scales[:, 0:P],
+                    rhs=w_codes[:, 0:BANK].bitcast(FP8X4),
+                    rhs_scale=w_scales[:, 0:BANK],
+                    start=True,
+                    stop=True,
+                )
+            if i == 2 and c_pass in (0, 1, 2):
                 nc.tensor.matmul(
-                    tp[:, 0:256], lhsT=ident_bf[:], rhs=k_sb[:, 0:256], start=True, stop=True
+                    tp[:, 0:512], lhsT=ident_bf[:], rhs=k_sb[:, 0:512], start=True, stop=True
                 )
             for u in range(2):
                 for a in range(2):
@@ -461,29 +474,44 @@ def tile_diffattn_pa_kernel(
             copy(out=o_sb[:], in_=turned[("out", b)][:, 0:H])
             nc.sync.dma_start(out=out_rows[b * P : (b + 1) * P, :], in_=o_sb[:])
 
+        idle = psum_s.tile([P, BANK], F32, tag="sc")
+        for i in range(4):
+            nc.tensor.matmul(
+                idle[:, 0:256], lhsT=warm_bf[:, 0:P], rhs=warm_bf[:, 0:256], start=True, stop=True
+            )
+
+        def keep_busy():
+            for i in range(2):
+                nc.tensor.matmul(
+                    idle[:, 0 : 2 * P], lhsT=warm_bf[:, 0:P], rhs=warm_bf[:], start=True, stop=True
+                )
+
         transpose_queries(1)
+        keep_busy()
         transpose_keys(0, 0)
         transpose_keys(0, 1)
-        transpose_queries(3)
+        keep_busy()
         copy_keys(0, 0, nc.vector.tensor_copy)
         copy_keys(0, 1, nc.vector.tensor_copy)
         copy_queries(1)
-        copy_queries(3)
-        transpose_keys(1, 0)
         scores(3, 0)
         scores(3, 1)
+        transpose_queries(3)
+        keep_busy()
+        transpose_keys(1, 0)
         lam_transpose()
         transpose_keys(1, 1)
-        copy_keys(1, 0, nc.vector.tensor_copy)
         bank_maximum(3, 0, 0)
-        negative_maximum(3, 0)
         bank_maximum(3, 1, 0)
-        copy_keys(1, 1, nc.scalar.copy)
+        negative_maximum(3, 0)
+        copy_keys(1, 0, nc.vector.tensor_copy)
+        negative_maximum(3, 1)
+        copy_queries(3)
         lam_columns()
         exps(3, 0)
+        copy_keys(1, 1, nc.scalar.copy)
         scores(7, 0)
         lam_products()
-        negative_maximum(3, 1)
         bank_maximum(7, 0, 0)
         bank_maximum(7, 0, 1)
         lam_sums()
@@ -494,14 +522,14 @@ def tile_diffattn_pa_kernel(
         words_onto_partitions(0, 1)
         words_onto_partitions(0, 2)
         words_onto_partitions(0, 3)
+        inverse_sums(3)
         lam_negative()
         negative_maximum(7, 0)
-        inverse_sums(3)
         scale_second(3)
         bank_maximum(7, 1, 0)
         bank_maximum(7, 1, 1)
-        negative_maximum(7, 1)
         combine(3)
+        negative_maximum(7, 1)
         regroup_words(0, 2, nc.vector.tensor_copy)
         regroup_words(0, 3, nc.vector.tensor_copy)
         exps(7, 0)
@@ -517,11 +545,11 @@ def tile_diffattn_pa_kernel(
         bank_maximum(6, 0, 0)
         bank_maximum(6, 0, 1)
         row_sums(7)
+        bank_maximum(6, 1, 0)
         negative_maximum(6, 0)
         inverse_sums(7)
-        bank_maximum(6, 1, 0)
-        scale_second(7)
         bank_maximum(6, 1, 1)
+        scale_second(7)
         regroup_words(1, 0, nc.scalar.copy)
         regroup_att(3)
         copy_queries(2)
@@ -547,11 +575,11 @@ def tile_diffattn_pa_kernel(
         words_onto_partitions(2, 2)
         words_onto_partitions(2, 3)
         row_sums(6)
+        bank_maximum(5, 1, 0)
         negative_maximum(5, 0)
         inverse_sums(6)
-        bank_maximum(5, 1, 0)
-        scale_second(6)
         bank_maximum(5, 1, 1)
+        scale_second(6)
         regroup_att(7)
         exps(5, 0)
         regroup_words(2, 1, nc.scalar.copy)
@@ -573,10 +601,9 @@ def tile_diffattn_pa_kernel(
         words_onto_partitions(3, 2)
         transpose_queries(0)
         row_sums(5)
+        bank_maximum(4, 1, 0)
         negative_maximum(4, 0)
         inverse_sums(5)
-        bank_maximum(4, 1, 0)
-        scale_second(5)
         bank_maximum(4, 1, 1)
         regroup_att(6)
         exps(4, 0)
@@ -586,6 +613,7 @@ def tile_diffattn_pa_kernel(
         scores(2, 0)
         words_onto_partitions(4, 0)
         quantise_att(6)
+        scale_second(5)
         negative_maximum(4, 1)
         combine(5)
         quantise_piece(2)
@@ -601,14 +629,13 @@ def tile_diffattn_pa_kernel(
         words_onto_partitions(4, 3)
         project_v(0, 0, psum_s, "sc")
         project_v(0, 1, psum_s, "sc")
+        bank_maximum(2, 1, 0)
         row_sums(4)
         negative_maximum(2, 0)
-        bank_maximum(2, 1, 0)
         inverse_sums(4)
         negative_maximum(2, 1)
         quantise_piece(3)
         scale_second(4)
-        combine(4)
         regroup_att(5)
         regroup_words(4, 1, nc.scalar.copy)
         regroup_words(4, 2, nc.scalar.copy)
@@ -619,62 +646,63 @@ def tile_diffattn_pa_kernel(
         regroup_v(0, 1)
         scores(1, 0)
         scores(1, 1)
-        transpose_att(4)
+        quantise_att(5)
         quantise_piece(4)
+        combine(4)
         bank_maximum(1, 0, 0)
         bank_maximum(1, 1, 0)
-        negative_maximum(1, 0)
         inverse_sums(2)
+        negative_maximum(1, 0)
+        quantise_v(0)
         negative_maximum(1, 1)
         scale_second(2)
-        quantise_att(5)
-        combine(2)
         exps(1, 0)
-        regroup_att(4)
-        exps(1, 1)
-        project_v(1, 0, psum_t, "tp")
+        transpose_att(4)
         scores(0, 0)
         scores(0, 1)
-        transpose_att(2)
-        project_v(1, 1, psum_t, "tp")
+        project_v(1, 0, psum_t, "tp")
         bank_maximum(0, 0, 0)
         bank_maximum(0, 1, 0)
+        combine(2)
         negative_maximum(0, 0)
-        quantise_v(0)
-        negative_maximum(0, 1)
-        inverse_sums(1)
-        scale_second(1)
-        quantise_att(4)
-        combine(1)
+        regroup_att(4)
+        exps(1, 1)
         exps(0, 0)
+        transpose_att(2)
+        project_v(1, 1, psum_t, "tp")
+        attention_output(3, psum_t, "tp")
+        inverse_sums(1)
+        negative_maximum(0, 1)
+        quantise_att(4)
+        scale_second(1)
         exps(0, 1)
         regroup_v(1, 0)
         regroup_att(2)
         regroup_v(1, 1)
-        transpose_att(1)
-        attention_output(3, psum_t, "tp")
         inverse_sums(0)
+        combine(1)
         scale_second(0)
-        quantise_att(2)
         combine(0)
-        quantise_v(1)
+        quantise_att(2)
         store_output(3, nc.vector.tensor_copy)
-        regroup_att(1)
+        quantise_v(1)
+        transpose_att(1)
+        attention_output(2, psum_t, "tp")
         transpose_att(0)
         attention_output(7, psum_s, "sc")
         attention_output(6, psum_s, "sc")
         attention_output(5, psum_s, "sc")
-        quantise_att(1)
-        store_output(6, nc.vector.tensor_copy)
+        attention_output(4, psum_s, "sc")
+        regroup_att(1)
         regroup_att(0)
+        store_output(2, nc.scalar.copy)
         store_output(7, nc.scalar.copy)
         store_output(5, nc.scalar.copy)
-        attention_output(4, psum_s, "sc")
-        attention_output(2, psum_s, "sc")
-        attention_output(1, psum_s, "sc")
+        quantise_att(1)
         quantise_att(0)
+        store_output(6, nc.vector.tensor_copy)
         store_output(4, nc.vector.tensor_copy)
+        attention_output(1, psum_t, "tp")
+        attention_output(0, psum_t, "tp")
         store_output(1, nc.vector.tensor_copy)
-        store_output(2, nc.scalar.copy)
-        attention_output(0, psum_s, "sc")
         store_output(0, nc.scalar.copy)

@@ -45,13 +45,19 @@ def tile_diffattn_pa_kernel(
     with ExitStack() as stack:
         keep = stack.enter_context(tc.tile_pool(name="keep", bufs=1))
         work = stack.enter_context(tc.tile_pool(name="work", bufs=3))
-        stats = stack.enter_context(tc.tile_pool(name="stats", bufs=5))
+        stats = stack.enter_context(tc.tile_pool(name="stats", bufs=8))
         psum_s = stack.enter_context(tc.psum_pool(name="psum_s", bufs=4))
         psum_t = stack.enter_context(tc.psum_pool(name="psum_t", bufs=4))
         stack.enter_context(tc.manual_schedule())
 
-        warm_bf = keep.tile([P, 2 * P], BF16, name="warm_bf")
-        nc.vector.memset(warm_bf[:], 0.0)
+        busy_tile = keep.tile([P, 2 * P], BF16, name="busy_tile")
+        nc.vector.memset(busy_tile[:], 0.0)
+
+        def keep_busy(bank):
+            for i in range(2):
+                nc.tensor.matmul(
+                    bank[:, 0 : 2 * P], lhsT=busy_tile[:, 0:P], rhs=busy_tile[:], start=True, stop=True
+                )
 
         k_sb = keep.tile([P, BLOCKS * H], BF16, name="k_sb")
         q_sb = keep.tile([P, BLOCKS * H], BF16, name="q_sb")
@@ -64,7 +70,7 @@ def tile_diffattn_pa_kernel(
 
         load_blocks(q_sb, q_rows, 2, 2)
         load_blocks(k_sb, k_rows, 0, 4)
-        load_blocks(q_sb, q_rows, 4, 4)
+        load_blocks(q_sb, q_rows, 6, 2)
         load_blocks(k_sb, k_rows, 4, 4)
 
         lam_rows = keep.tile([P, P], BF16, name="lam_rows")
@@ -79,6 +85,8 @@ def tile_diffattn_pa_kernel(
             out=w_sb[:].rearrange("p (a c) -> p a c", a=2),
             in_=Wv.rearrange("(a p) c -> p a c", p=P),
         )
+        load_blocks(q_sb, q_rows, 4, 2)
+
         x_sb = [keep.tile([P, 2 * C], BF16, name="x_sb%d" % j) for j in range(PAIRS)]
         for j in range(PAIRS):
             nc.sync.dma_start(
@@ -223,7 +231,9 @@ def tile_diffattn_pa_kernel(
             src_words = piece_rows[i][:].bitcast(F32)
             tp = psum_t.tile([P, BANK], F32, tag="tp")
             turned[(i, c_pass)] = tp
-            if i > 2 and c_pass % 2 == 0:
+            if i == 2 and c_pass < 3:
+                keep_busy(tp)
+            if i > 2 and c_pass < 2:
                 nc.tensor.matmul_mx(
                     out=tp[:],
                     lhsT=w_codes[:, 0:P].bitcast(FP8X4),
@@ -232,10 +242,6 @@ def tile_diffattn_pa_kernel(
                     rhs_scale=w_scales[:, 0:BANK],
                     start=True,
                     stop=True,
-                )
-            if i == 2 and c_pass in (0, 1, 2):
-                nc.tensor.matmul(
-                    tp[:, 0:512], lhsT=ident_bf[:], rhs=k_sb[:, 0:512], start=True, stop=True
                 )
             for u in range(2):
                 for a in range(2):
@@ -309,48 +315,72 @@ def tile_diffattn_pa_kernel(
         row_sum_tiles = {}
         seconds = {}
 
+        def masked_scores(dst, b, h, first, width):
+            queries = qT[:, h * T + b * P : h * T + (b + 1) * P]
+            before = width - P
+            nc.tensor.matmul(
+                dst[:, before:width], lhsT=ident_bf[:], rhs=mask_bf[:], start=True, stop=False
+            )
+            nc.tensor.matmul(
+                dst[:, before:width],
+                lhsT=queries,
+                rhs=kT[:, h * T + first + before : h * T + first + width],
+                start=False,
+                stop=True,
+            )
+            if before > 0:
+                nc.tensor.matmul(
+                    dst[:, 0:before],
+                    lhsT=queries,
+                    rhs=kT[:, h * T + first : h * T + first + before],
+                    start=True,
+                    stop=True,
+                )
+
         def scores(b, h):
             keys = (b + 1) * P
-            banks = key_passes_of[b]
-            queries = qT[:, h * T + b * P : h * T + (b + 1) * P]
-            score_banks[(b, h)] = []
-            for c in reversed(range(banks)):
-                first = c * BANK
-                width = min(keys - first, BANK)
+            first = (key_passes_of[b] - 1) * BANK
+            sc = psum_s.tile([P, BANK], F32, tag="sc")
+            masked_scores(sc, b, h, first, keys - first)
+            score_banks[(b, h)] = [(sc[:, 0 : keys - first], first, keys - first)]
+            if first > 0:
                 sc = psum_s.tile([P, BANK], F32, tag="sc")
-                score_banks[(b, h)].append((sc, first, width))
-                before = width - P if c == banks - 1 else width
-                if c == banks - 1:
-                    nc.tensor.matmul(
-                        sc[:, before:width], lhsT=ident_bf[:], rhs=mask_bf[:], start=True, stop=False
-                    )
-                    nc.tensor.matmul(
-                        sc[:, before:width],
-                        lhsT=queries,
-                        rhs=kT[:, h * T + first + before : h * T + first + width],
-                        start=False,
-                        stop=True,
-                    )
-                if before > 0:
-                    nc.tensor.matmul(
-                        sc[:, 0:before],
-                        lhsT=queries,
-                        rhs=kT[:, h * T + first : h * T + first + before],
-                        start=True,
-                        stop=True,
-                    )
+                nc.tensor.matmul(
+                    sc[:],
+                    lhsT=qT[:, h * T + b * P : h * T + (b + 1) * P],
+                    rhs=kT[:, h * T : h * T + BANK],
+                    start=True,
+                    stop=True,
+                )
+                score_banks[(b, h)].append((sc[:], 0, BANK))
+
+        def scores_of_both_heads(b):
+            keys = (b + 1) * P
+            sc = psum_s.tile([P, BANK], F32, tag="sc")
+            turned[("scores", b)] = sc
+            for h in range(2):
+                masked_scores(sc[:, h * keys : (h + 1) * keys], b, h, 0, keys)
+                score_banks[(b, h)] = [(sc[:, h * keys : (h + 1) * keys], 0, keys)]
+
+        def row_statistics(b):
+            bank_max = stats.tile([P, 4], F32, tag="bank_max")
+            neg_max = stats.tile([P, 2], F32, tag="neg_max")
+            bank_sum = stats.tile([P, 4], F32, tag="bank_sum")
+            stat_tiles[b] = (bank_max, neg_max, bank_sum)
 
         def bank_maximum(b, h, c):
-            if b not in stat_tiles:
-                bank_max = stats.tile([P, 4], F32, tag="bank_max")
-                neg_max = stats.tile([P, 2], F32, tag="neg_max")
-                bank_sum = stats.tile([P, 4], F32, tag="bank_sum")
-                stat_tiles[b] = (bank_max, neg_max, bank_sum)
             bank_max, neg_max, bank_sum = stat_tiles[b]
             sc, first, width = score_banks[(b, h)][c]
             nc.vector.tensor_reduce(
-                out=bank_max[:, 2 * h + c : 2 * h + c + 1],
-                in_=sc[:, 0:width],
+                out=bank_max[:, 2 * h + c : 2 * h + c + 1], in_=sc, axis=AXIS_X, op=ALU.max
+            )
+
+        def maxima_of_both_heads(b):
+            bank_max, neg_max, bank_sum = stat_tiles[b]
+            keys = (b + 1) * P
+            nc.vector.tensor_reduce(
+                out=bank_max[:, 0:4:2],
+                in_=turned[("scores", b)][:, 0 : 2 * keys].rearrange("p (h k) -> p h k", h=2),
                 axis=AXIS_X,
                 op=ALU.max,
             )
@@ -365,15 +395,25 @@ def tile_diffattn_pa_kernel(
                     scalar2=None,
                     op0=ALU.mult,
                 )
-            else:
-                nc.vector.tensor_scalar(
-                    out=neg_max[:, h : h + 1],
-                    in0=bank_max[:, 2 * h : 2 * h + 1],
-                    scalar1=bank_max[:, 2 * h + 1 : 2 * h + 2],
-                    scalar2=-SCALE,
-                    op0=ALU.max,
-                    op1=ALU.mult,
-                )
+                return
+            nc.vector.tensor_scalar(
+                out=neg_max[:, h : h + 1],
+                in0=bank_max[:, 2 * h : 2 * h + 1],
+                scalar1=bank_max[:, 2 * h + 1 : 2 * h + 2],
+                scalar2=-SCALE,
+                op0=ALU.max,
+                op1=ALU.mult,
+            )
+
+        def negative_maxima(b):
+            bank_max, neg_max, bank_sum = stat_tiles[b]
+            nc.vector.tensor_scalar(
+                out=neg_max[:],
+                in0=bank_max[:, 0:4:2],
+                scalar1=-SCALE,
+                scalar2=None,
+                op0=ALU.mult,
+            )
 
         def exps(b, h):
             if b not in exp_tiles:
@@ -383,7 +423,7 @@ def tile_diffattn_pa_kernel(
             for c, (sc, first, width) in enumerate(score_banks[(b, h)]):
                 nc.scalar.activation(
                     out=exp_tiles[b][:, h * T + first : h * T + first + width],
-                    in_=sc[:, 0:width],
+                    in_=sc,
                     func=ACT.Exp,
                     bias=neg_max[:, h : h + 1],
                     scale=SCALE,
@@ -474,54 +514,55 @@ def tile_diffattn_pa_kernel(
             copy(out=o_sb[:], in_=turned[("out", b)][:, 0:H])
             nc.sync.dma_start(out=out_rows[b * P : (b + 1) * P, :], in_=o_sb[:])
 
-        idle = psum_s.tile([P, BANK], F32, tag="sc")
-        for i in range(4):
-            nc.tensor.matmul(
-                idle[:, 0:256], lhsT=warm_bf[:, 0:P], rhs=warm_bf[:, 0:256], start=True, stop=True
-            )
+        on_vector = nc.vector.tensor_copy
+        on_scalar = nc.scalar.copy
+        ORDER = [3, 7, 6, 5, 4, 2, 1, 0]
 
-        def keep_busy():
-            for i in range(2):
-                nc.tensor.matmul(
-                    idle[:, 0 : 2 * P], lhsT=warm_bf[:, 0:P], rhs=warm_bf[:], start=True, stop=True
-                )
+        def regroup_unit(n, copy):
+            regroup_words(n // C_PASSES, n % C_PASSES, copy)
+
+        for b in ORDER:
+            row_statistics(b)
+
+        idle = psum_s.tile([P, BANK], F32, tag="sc")
+        keep_busy(idle)
+        keep_busy(idle)
+        keep_busy(idle)
 
         transpose_queries(1)
-        keep_busy()
         transpose_keys(0, 0)
         transpose_keys(0, 1)
-        keep_busy()
-        copy_keys(0, 0, nc.vector.tensor_copy)
-        copy_keys(0, 1, nc.vector.tensor_copy)
+        transpose_queries(3)
+        keep_busy(idle)
         copy_queries(1)
+        copy_keys(0, 0, on_vector)
+        copy_keys(0, 1, on_vector)
         scores(3, 0)
         scores(3, 1)
-        transpose_queries(3)
-        keep_busy()
+        copy_queries(3)
         transpose_keys(1, 0)
         lam_transpose()
         transpose_keys(1, 1)
+        keep_busy(idle)
         bank_maximum(3, 0, 0)
         bank_maximum(3, 1, 0)
         negative_maximum(3, 0)
-        copy_keys(1, 0, nc.vector.tensor_copy)
         negative_maximum(3, 1)
-        copy_queries(3)
+        copy_keys(1, 0, on_scalar)
+        copy_keys(1, 1, on_scalar)
         lam_columns()
         exps(3, 0)
-        copy_keys(1, 1, nc.scalar.copy)
-        scores(7, 0)
+        exps(3, 1)
         lam_products()
-        bank_maximum(7, 0, 0)
-        bank_maximum(7, 0, 1)
+        scores(7, 0)
         lam_sums()
         lam_exps()
-        exps(3, 1)
         scores(7, 1)
-        words_onto_partitions(0, 0)
-        words_onto_partitions(0, 1)
-        words_onto_partitions(0, 2)
-        words_onto_partitions(0, 3)
+        for c_pass in range(C_PASSES):
+            words_onto_partitions(0, c_pass)
+
+        bank_maximum(7, 0, 0)
+        bank_maximum(7, 0, 1)
         inverse_sums(3)
         lam_negative()
         negative_maximum(7, 0)
@@ -530,179 +571,120 @@ def tile_diffattn_pa_kernel(
         bank_maximum(7, 1, 1)
         combine(3)
         negative_maximum(7, 1)
-        regroup_words(0, 2, nc.vector.tensor_copy)
-        regroup_words(0, 3, nc.vector.tensor_copy)
         exps(7, 0)
-        regroup_words(0, 0, nc.scalar.copy)
-        regroup_words(0, 1, nc.scalar.copy)
-        exps(7, 1)
         scores(6, 0)
+        regroup_unit(0, on_scalar)
+        regroup_unit(1, on_scalar)
+        regroup_unit(2, on_vector)
+        regroup_unit(3, on_vector)
         words_onto_partitions(1, 0)
         transpose_att(3)
+        exps(7, 1)
         scores(6, 1)
+        regroup_unit(4, on_scalar)
         transpose_queries(2)
-        words_onto_partitions(1, 1)
-        bank_maximum(6, 0, 0)
-        bank_maximum(6, 0, 1)
-        row_sums(7)
-        bank_maximum(6, 1, 0)
-        negative_maximum(6, 0)
-        inverse_sums(7)
-        bank_maximum(6, 1, 1)
-        scale_second(7)
-        regroup_words(1, 0, nc.scalar.copy)
+        for c_pass in range(1, C_PASSES):
+            words_onto_partitions(1, c_pass)
         regroup_att(3)
         copy_queries(2)
-        exps(6, 0)
-        regroup_words(1, 1, nc.scalar.copy)
-        words_onto_partitions(1, 2)
-        words_onto_partitions(1, 3)
-        scores(5, 0)
-        words_onto_partitions(2, 0)
-        quantise_att(3)
-        negative_maximum(6, 1)
-        combine(7)
-        quantise_piece(0)
-        bank_maximum(5, 0, 0)
-        bank_maximum(5, 0, 1)
-        regroup_words(1, 2, nc.scalar.copy)
-        exps(6, 1)
-        regroup_words(1, 3, nc.scalar.copy)
-        regroup_words(2, 0, nc.scalar.copy)
-        transpose_att(7)
-        scores(5, 1)
-        words_onto_partitions(2, 1)
-        words_onto_partitions(2, 2)
-        words_onto_partitions(2, 3)
-        row_sums(6)
-        bank_maximum(5, 1, 0)
-        negative_maximum(5, 0)
-        inverse_sums(6)
-        bank_maximum(5, 1, 1)
-        scale_second(6)
-        regroup_att(7)
-        exps(5, 0)
-        regroup_words(2, 1, nc.scalar.copy)
-        regroup_words(2, 2, nc.scalar.copy)
-        words_onto_partitions(3, 0)
-        scores(4, 0)
-        quantise_att(7)
-        negative_maximum(5, 1)
-        combine(6)
-        quantise_piece(1)
-        bank_maximum(4, 0, 0)
-        bank_maximum(4, 0, 1)
-        exps(5, 1)
-        regroup_words(2, 3, nc.scalar.copy)
-        regroup_words(3, 0, nc.scalar.copy)
-        transpose_att(6)
-        words_onto_partitions(3, 1)
-        scores(4, 1)
-        words_onto_partitions(3, 2)
-        transpose_queries(0)
-        row_sums(5)
-        bank_maximum(4, 1, 0)
-        negative_maximum(4, 0)
-        inverse_sums(5)
-        bank_maximum(4, 1, 1)
-        regroup_att(6)
-        exps(4, 0)
-        regroup_words(3, 1, nc.scalar.copy)
-        regroup_words(3, 2, nc.scalar.copy)
-        words_onto_partitions(3, 3)
-        scores(2, 0)
-        words_onto_partitions(4, 0)
-        quantise_att(6)
-        scale_second(5)
-        negative_maximum(4, 1)
-        combine(5)
-        quantise_piece(2)
+
+        for step in range(2, 5):
+            before, last, cur, nxt = ORDER[step - 2 : step + 2]
+            piece = step
+            unit = 4 * step - 3
+            bank_maximum(cur, 0, 0)
+            bank_maximum(cur, 0, 1)
+            row_sums(last)
+            bank_maximum(cur, 1, 0)
+            negative_maximum(cur, 0)
+            inverse_sums(last)
+            bank_maximum(cur, 1, 1)
+            scale_second(last)
+            quantise_att(before)
+            negative_maximum(cur, 1)
+            combine(last)
+            quantise_piece(piece - 2)
+
+            exps(cur, 0)
+            scores(nxt, 0)
+            regroup_unit(unit, on_scalar)
+            regroup_unit(unit + 1, on_scalar)
+            words_onto_partitions(piece, 0)
+            transpose_att(last)
+            exps(cur, 1)
+            scores(nxt, 1)
+            regroup_unit(unit + 2, on_scalar)
+            regroup_unit(unit + 3, on_scalar)
+            for c_pass in range(1, C_PASSES):
+                words_onto_partitions(piece, c_pass)
+            regroup_att(last)
+
         bank_maximum(2, 0, 0)
-        exps(4, 1)
-        copy_queries(0)
-        regroup_words(3, 3, nc.scalar.copy)
-        regroup_words(4, 0, nc.scalar.copy)
-        transpose_att(5)
-        scores(2, 1)
-        words_onto_partitions(4, 1)
-        words_onto_partitions(4, 2)
-        words_onto_partitions(4, 3)
-        project_v(0, 0, psum_s, "sc")
-        project_v(0, 1, psum_s, "sc")
-        bank_maximum(2, 1, 0)
         row_sums(4)
-        negative_maximum(2, 0)
+        bank_maximum(2, 1, 0)
         inverse_sums(4)
-        negative_maximum(2, 1)
         quantise_piece(3)
+        negative_maxima(2)
         scale_second(4)
-        regroup_att(5)
-        regroup_words(4, 1, nc.scalar.copy)
-        regroup_words(4, 2, nc.scalar.copy)
-        regroup_words(4, 3, nc.scalar.copy)
+        quantise_att(5)
+        project_v(0, 0, psum_s, "sc")
+        transpose_queries(0)
+        project_v(0, 1, psum_s, "sc")
+        for n in range(17, 20):
+            regroup_unit(n, on_scalar)
         regroup_v(0, 0)
+        copy_queries(0)
         exps(2, 0)
         exps(2, 1)
         regroup_v(0, 1)
-        scores(1, 0)
-        scores(1, 1)
-        quantise_att(5)
         quantise_piece(4)
         combine(4)
-        bank_maximum(1, 0, 0)
-        bank_maximum(1, 1, 0)
-        inverse_sums(2)
-        negative_maximum(1, 0)
-        quantise_v(0)
-        negative_maximum(1, 1)
-        scale_second(2)
-        exps(1, 0)
+        scores_of_both_heads(1)
         transpose_att(4)
-        scores(0, 0)
-        scores(0, 1)
-        project_v(1, 0, psum_t, "tp")
-        bank_maximum(0, 0, 0)
-        bank_maximum(0, 1, 0)
+        scores_of_both_heads(0)
+        maxima_of_both_heads(1)
+        inverse_sums(2)
+        quantise_v(0)
+        negative_maxima(1)
+        scale_second(2)
+        maxima_of_both_heads(0)
         combine(2)
-        negative_maximum(0, 0)
+        negative_maxima(0)
+        exps(1, 0)
         regroup_att(4)
         exps(1, 1)
         exps(0, 0)
+        exps(0, 1)
+        project_v(1, 0, psum_t, "tp")
         transpose_att(2)
         project_v(1, 1, psum_t, "tp")
-        attention_output(3, psum_t, "tp")
-        inverse_sums(1)
-        negative_maximum(0, 1)
         quantise_att(4)
+        inverse_sums(1)
+        inverse_sums(0)
         scale_second(1)
-        exps(0, 1)
+        scale_second(0)
+        combine(1)
+        combine(0)
         regroup_v(1, 0)
         regroup_att(2)
         regroup_v(1, 1)
-        inverse_sums(0)
-        combine(1)
-        scale_second(0)
-        combine(0)
-        quantise_att(2)
-        store_output(3, nc.vector.tensor_copy)
-        quantise_v(1)
+        attention_output(3, psum_t, "tp")
         transpose_att(1)
-        attention_output(2, psum_t, "tp")
-        transpose_att(0)
-        attention_output(7, psum_s, "sc")
-        attention_output(6, psum_s, "sc")
-        attention_output(5, psum_s, "sc")
-        attention_output(4, psum_s, "sc")
         regroup_att(1)
+        transpose_att(0)
+        quantise_att(2)
+        attention_output(2, psum_t, "tp")
+        store_output(3, on_vector)
+        quantise_v(1)
         regroup_att(0)
-        store_output(2, nc.scalar.copy)
-        store_output(7, nc.scalar.copy)
-        store_output(5, nc.scalar.copy)
         quantise_att(1)
         quantise_att(0)
-        store_output(6, nc.vector.tensor_copy)
-        store_output(4, nc.vector.tensor_copy)
+        for b in (7, 6, 5, 4):
+            attention_output(b, psum_s, "sc")
         attention_output(1, psum_t, "tp")
         attention_output(0, psum_t, "tp")
-        store_output(1, nc.vector.tensor_copy)
-        store_output(0, nc.scalar.copy)
+        store_output(2, on_scalar)
+        for b, copy in ((7, on_scalar), (6, on_vector), (5, on_scalar), (4, on_vector)):
+            store_output(b, copy)
+        store_output(1, on_vector)
+        store_output(0, on_scalar)

@@ -640,8 +640,9 @@ def tile_diffattn_pa_kernel(
         quantise_piece(4)
         combine(4)
         scores_of_both_heads(1)
-        transpose_att(4)
         scores_of_both_heads(0)
+        project_v(1, 0, psum_t, "tp")
+        transpose_att(4)
         maxima_of_both_heads(1)
         inverse_sums(2)
         quantise_v(0)
@@ -651,21 +652,20 @@ def tile_diffattn_pa_kernel(
         combine(2)
         negative_maxima(0)
         exps(1, 0)
-        regroup_att(4)
         exps(1, 1)
         exps(0, 0)
         exps(0, 1)
-        project_v(1, 0, psum_t, "tp")
+        regroup_v(1, 0)
+        regroup_att(4)
         transpose_att(2)
         project_v(1, 1, psum_t, "tp")
-        quantise_att(4)
         inverse_sums(1)
         inverse_sums(0)
         scale_second(1)
         scale_second(0)
         combine(1)
+        quantise_att(4)
         combine(0)
-        regroup_v(1, 0)
         regroup_att(2)
         regroup_v(1, 1)
         attention_output(3, psum_t, "tp")

import math
from contextlib import ExitStack

import concourse.mybir as mybir
from concourse.masks import make_identity

BF16 = mybir.dt.bfloat16
F32 = mybir.dt.float32
U32 = mybir.dt.uint32
U8 = mybir.dt.uint8
FP8X4 = mybir.dt.float8_e4m3fn_x4
ALU = mybir.AluOpType
ACT = mybir.ActivationFunctionType
AXIS_X = mybir.AxisListType.X

P = 128
T = 1024
C = 2048
H = 256
D = 128
K_PASS = 512
BANK = 512
BLOCKS = T // P
PAIRS = T // (2 * P)
C_PASSES = C // K_PASS
KEY_PASSES = T // K_PASS

SCALE = 1.0 / math.sqrt(D)
LAMBDA_INIT = 0.8 - 0.6 * math.exp(-0.3)
MASKED = -1.0e30

CAUSAL_PAIRS = 512 * 512 + 512 * 1024
FLOPS = 2 * T * C * H + 2 * 2 * CAUSAL_PAIRS * D + 2 * CAUSAL_PAIRS * H


def tile_diffattn_pa_kernel(
    tc, q, k, x, Wv, lambda_q1, lambda_q2, lambda_k1, lambda_k2, out
):
    nc = tc.nc
    q_rows = q.flatten_outer_dims()
    k_rows = k.flatten_outer_dims()
    x_rows = x.flatten_outer_dims()
    out_rows = out.flatten_outer_dims()

    with ExitStack() as stack:
        keep = stack.enter_context(tc.tile_pool(name="keep", bufs=1))
        work = stack.enter_context(tc.tile_pool(name="work", bufs=3))
        stats = stack.enter_context(tc.tile_pool(name="stats", bufs=8))
        psum_s = stack.enter_context(tc.psum_pool(name="psum_s", bufs=4))
        psum_t = stack.enter_context(tc.psum_pool(name="psum_t", bufs=4))
        stack.enter_context(tc.manual_schedule())

        busy_tile = keep.tile([P, 2 * P], BF16, name="busy_tile")
        nc.vector.memset(busy_tile[:], 0.0)

        def keep_busy(bank):
            for i in range(2):
                nc.tensor.matmul(
                    bank[:, 0 : 2 * P], lhsT=busy_tile[:, 0:P], rhs=busy_tile[:], start=True, stop=True
                )

        k_sb = keep.tile([P, BLOCKS * H], BF16, name="k_sb")
        q_sb = keep.tile([P, BLOCKS * H], BF16, name="q_sb")

        def load_blocks(dst, rows, first, count):
            nc.sync.dma_start(
                out=dst[:, first * H : (first + count) * H].rearrange("p (b d) -> p b d", d=H),
                in_=rows[first * P : (first + count) * P, :].rearrange("(b p) d -> p b d", p=P),
            )

        load_blocks(q_sb, q_rows, 2, 2)
        load_blocks(k_sb, k_rows, 0, 4)
        load_blocks(q_sb, q_rows, 6, 2)
        load_blocks(k_sb, k_rows, 4, 4)

        lam_rows = keep.tile([P, P], BF16, name="lam_rows")
        nc.vector.memset(lam_rows[:], 0.0)
        for r, vec in enumerate((lambda_q1, lambda_q2, lambda_k1, lambda_k2)):
            nc.sync.dma_start(
                out=lam_rows[r : r + 1, :], in_=vec.rearrange("(o d) -> o d", o=1)
            )

        w_sb = keep.tile([P, 2 * C], BF16, name="w_sb")
        nc.sync.dma_start(
            out=w_sb[:].rearrange("p (a c) -> p a c", a=2),
            in_=Wv.rearrange("(a p) c -> p a c", p=P),
        )
        load_blocks(q_sb, q_rows, 4, 2)

        x_sb = [keep.tile([P, 2 * C], BF16, name="x_sb%d" % j) for j in range(PAIRS)]
        for j in range(PAIRS):
            nc.sync.dma_start(
                out=x_sb[j][:],
                in_=x_rows[j * 2 * P : (j + 1) * 2 * P, :].rearrange("(p e) c -> p (e c)", e=2),
            )
        load_blocks(q_sb, q_rows, 0, 2)

        ones_f32 = keep.tile([P, P], F32, name="ones_f32")
        nc.vector.memset(ones_f32[:], 1.0)

        warm = keep.tile([P, 1], F32, name="warm")
        nc.scalar.activation(out=warm[:], in_=ones_f32[:, 0:1], func=ACT.Exp)
        ident_bf = keep.tile([P, P], BF16, name="ident_bf")
        make_identity(nc, ident_bf[:])
        ident_f32 = keep.tile([P, P], F32, name="ident_f32")
        make_identity(nc, ident_f32[:])
        mask_f32 = keep.tile([P, P], F32, name="mask_f32")
        nc.gpsimd.memset(mask_f32[:], 0.0)
        nc.gpsimd.affine_select(
            out=mask_f32[:],
            in_=mask_f32[:],
            compare_op=ALU.is_ge,
            fill=MASKED,
            base=0,
            pattern=[[-1, P]],
            channel_multiplier=1,
        )
        mask_bf = keep.tile([P, P], BF16, name="mask_bf")
        nc.vector.tensor_copy(out=mask_bf[:], in_=mask_f32[:])

        key_passes_of = [b // 4 + 1 for b in range(BLOCKS)]
        att = [
            keep.tile([P, key_passes_of[b] * K_PASS], BF16, name="att%d" % b)
            for b in range(BLOCKS)
        ]
        att_grouped = [
            keep.tile([P, key_passes_of[b] * K_PASS], BF16, name="att_grouped%d" % b, align_bytes=64)
            for b in range(BLOCKS)
        ]
        att_codes = [
            keep.tile([P, key_passes_of[b] * P], U32, name="att_codes%d" % b, align_bytes=64)
            for b in range(BLOCKS)
        ]
        att_scales = [
            keep.tile([P, key_passes_of[b] * P], U8, name="att_scales%d" % b, align_bytes=64)
            for b in range(BLOCKS)
        ]
        for b in range(BLOCKS):
            if (b + 1) * P < key_passes_of[b] * K_PASS:
                nc.gpsimd.memset(att[b][:, (b + 1) * P :], 0.0)

        kT = keep.tile([P, 2 * T], BF16, name="kT")
        qT = keep.tile([P, 2 * T], BF16, name="qT")
        turned = {}

        def transpose_keys(half, h):
            tp = psum_t.tile([P, BANK], BF16, tag="tp")
            turned[("k", half, h)] = tp
            for i in range(4):
                b = half * 4 + i
                nc.tensor.transpose(
                    tp[:, i * P : (i + 1) * P],
                    k_sb[:, b * H + h * D : b * H + (h + 1) * D],
                    ident_bf[:],
                )

        def copy_keys(half, h, copy):
            copy(
                out=kT[:, h * T + half * 512 : h * T + (half + 1) * 512],
                in_=turned[("k", half, h)][:],
            )

        def transpose_queries(pair):
            tp = psum_t.tile([P, BANK], BF16, tag="tp")
            turned[("q", pair)] = tp
            for h in range(2):
                for i in range(2):
                    b = 2 * pair + i
                    nc.tensor.transpose(
                        tp[:, (2 * h + i) * P : (2 * h + i + 1) * P],
                        q_sb[:, b * H + h * D : b * H + (h + 1) * D],
                        ident_bf[:],
                    )

        def copy_queries(pair):
            nc.scalar.copy(
                out=qT[:].rearrange("p (h t) -> p h t", h=2)[:, :, 2 * pair * P : (2 * pair + 2) * P],
                in_=turned[("q", pair)][:].rearrange("p (h t) -> p h t", h=2),
            )

        neg_lam = keep.tile([P, 1], F32, name="neg_lam")
        lam_cols = keep.tile([P, 4], F32, name="lam_cols")
        lam_prod = keep.tile([P, 2], F32, name="lam_prod")
        lam_exp = keep.tile([P, 2], F32, name="lam_exp")

        def lam_transpose():
            lam_t = psum_t.tile([P, BANK], BF16, tag="tp")
            turned["lam"] = lam_t
            nc.tensor.transpose(lam_t[:, 0:P], lam_rows[:], ident_bf[:])

        def lam_columns():
            nc.scalar.copy(out=lam_cols[:], in_=turned["lam"][:, 0:4])

        def lam_products():
            nc.vector.tensor_mul(out=lam_prod[:], in0=lam_cols[:, 0:2], in1=lam_cols[:, 2:4])

        def lam_sums():
            lam_dot = psum_t.tile([P, BANK], F32, tag="tp")
            turned["dot"] = lam_dot
            nc.tensor.matmul(
                lam_dot[:, 0:2], lhsT=ones_f32[:], rhs=lam_prod[:], start=True, stop=True
            )

        def lam_exps():
            nc.scalar.activation(out=lam_exp[:], in_=turned["dot"][:, 0:2], func=ACT.Exp)

        def lam_negative():
            nc.vector.tensor_scalar(
                out=neg_lam[:],
                in0=lam_exp[:, 1:2],
                scalar1=lam_exp[:, 0:1],
                scalar2=LAMBDA_INIT,
                op0=ALU.subtract,
                op1=ALU.subtract,
            )

        GROUP_WORDS = C_PASSES * 2 * P
        w_grouped = keep.tile([P, GROUP_WORDS * 4], BF16, name="w_grouped", align_bytes=64)
        w_codes = keep.tile([P, GROUP_WORDS], U32, name="w_codes", align_bytes=64)
        w_scales = keep.tile([P, GROUP_WORDS], U8, name="w_scales", align_bytes=64)
        x_grouped = [
            keep.tile([P, GROUP_WORDS * 4], BF16, name="x_grouped%d" % j, align_bytes=64)
            for j in range(PAIRS)
        ]
        x_codes = keep.tile([P, PAIRS * GROUP_WORDS], U32, name="x_codes", align_bytes=64)
        x_scales = keep.tile([P, PAIRS * GROUP_WORDS], U8, name="x_scales", align_bytes=64)
        piece_rows = [w_sb] + x_sb
        piece_grouped = [w_grouped] + x_grouped

        def words_onto_partitions(i, c_pass):
            src_words = piece_rows[i][:].bitcast(F32)
            tp = psum_t.tile([P, BANK], F32, tag="tp")
            turned[(i, c_pass)] = tp
            if i == 2 and c_pass < 3:
                keep_busy(tp)
            if i > 2 and c_pass < 2:
                nc.tensor.matmul_mx(
                    out=tp[:],
                    lhsT=w_codes[:, 0:P].bitcast(FP8X4),
                    lhsT_scale=w_scales[:, 0:P],
                    rhs=w_codes[:, 0:BANK].bitcast(FP8X4),
                    rhs_scale=w_scales[:, 0:BANK],
                    start=True,
                    stop=True,
                )
            for u in range(2):
                for a in range(2):
                    first = a * (C // 2) + (2 * c_pass + u) * P
                    nc.tensor.transpose(
                        tp[:, (u * 2 + a) * P : (u * 2 + a + 1) * P],
                        src_words[:, first : first + P],
                        ident_f32[:],
                    )

        def regroup_words(i, c_pass, copy):
            copy(
                out=piece_grouped[i][:]
                .bitcast(F32)[:, c_pass * BANK : (c_pass + 1) * BANK]
                .rearrange("p (n u) -> p n u", u=2),
                in_=turned[(i, c_pass)][:].rearrange("p (u n) -> p n u", u=2),
            )

        def quantise_piece(i):
            if i == 0:
                nc.vector.quantize_mx(
                    out=w_codes[:].bitcast(FP8X4), scales=w_scales[:], in_=w_grouped[:]
                )
            else:
                cols = slice((i - 1) * GROUP_WORDS, i * GROUP_WORDS)
                nc.vector.quantize_mx(
                    out=x_codes[:, cols].bitcast(FP8X4),
                    scales=x_scales[:, cols],
                    in_=x_grouped[i - 1][:],
                )

        v_grouped = keep.tile([P, KEY_PASSES * H * 4], BF16, name="v_grouped", align_bytes=64)
        v_codes = keep.tile([P, KEY_PASSES * H], U32, name="v_codes", align_bytes=64)
        v_scales = keep.tile([P, KEY_PASSES * H], U8, name="v_scales", align_bytes=64)

        def project_v(g, half, pool, tag):
            acc = pool.tile([P, BANK], F32, tag=tag)
            turned[("v", g, half)] = acc
            for t in range(4):
                for c_pass in range(C_PASSES):
                    x_first = ((2 * g + t // 2) * C_PASSES + c_pass) * 2 * P + (t % 2) * P
                    w_first = c_pass * H + half * P
                    nc.tensor.matmul_mx(
                        out=acc[:, t * P : (t + 1) * P],
                        lhsT=x_codes[:, x_first : x_first + P].bitcast(FP8X4),
                        lhsT_scale=x_scales[:, x_first : x_first + P],
                        rhs=w_codes[:, w_first : w_first + P].bitcast(FP8X4),
                        rhs_scale=w_scales[:, w_first : w_first + P],
                        start=(c_pass == 0),
                        stop=(c_pass == C_PASSES - 1),
                    )

        def regroup_v(g, half):
            first = (g * 2 + half) * BANK
            nc.scalar.copy(
                out=v_grouped[:, first : first + BANK].rearrange("p (n t) -> p n t", t=4),
                in_=turned[("v", g, half)][:].rearrange("p (t n) -> p n t", t=4),
            )

        def quantise_v(g):
            nc.vector.quantize_mx(
                out=v_codes[:, g * H : (g + 1) * H].bitcast(FP8X4),
                scales=v_scales[:, g * H : (g + 1) * H],
                in_=v_grouped[:, g * H * 4 : (g + 1) * H * 4],
            )

        score_banks = {}
        stat_tiles = {}
        exp_tiles = {}
        inv_sums = {}
        row_sum_tiles = {}
        seconds = {}

        def masked_scores(dst, b, h, first, width):
            queries = qT[:, h * T + b * P : h * T + (b + 1) * P]
            before = width - P
            nc.tensor.matmul(
                dst[:, before:width], lhsT=ident_bf[:], rhs=mask_bf[:], start=True, stop=False
            )
            nc.tensor.matmul(
                dst[:, before:width],
                lhsT=queries,
                rhs=kT[:, h * T + first + before : h * T + first + width],
                start=False,
                stop=True,
            )
            if before > 0:
                nc.tensor.matmul(
                    dst[:, 0:before],
                    lhsT=queries,
                    rhs=kT[:, h * T + first : h * T + first + before],
                    start=True,
                    stop=True,
                )

        def scores(b, h):
            keys = (b + 1) * P
            first = (key_passes_of[b] - 1) * BANK
            sc = psum_s.tile([P, BANK], F32, tag="sc")
            masked_scores(sc, b, h, first, keys - first)
            score_banks[(b, h)] = [(sc[:, 0 : keys - first], first, keys - first)]
            if first > 0:
                sc = psum_s.tile([P, BANK], F32, tag="sc")
                nc.tensor.matmul(
                    sc[:],
                    lhsT=qT[:, h * T + b * P : h * T + (b + 1) * P],
                    rhs=kT[:, h * T : h * T + BANK],
                    start=True,
                    stop=True,
                )
                score_banks[(b, h)].append((sc[:], 0, BANK))

        def scores_of_both_heads(b):
            keys = (b + 1) * P
            sc = psum_s.tile([P, BANK], F32, tag="sc")
            turned[("scores", b)] = sc
            for h in range(2):
                masked_scores(sc[:, h * keys : (h + 1) * keys], b, h, 0, keys)
                score_banks[(b, h)] = [(sc[:, h * keys : (h + 1) * keys], 0, keys)]

        def row_statistics(b):
            bank_max = stats.tile([P, 4], F32, tag="bank_max")
            neg_max = stats.tile([P, 2], F32, tag="neg_max")
            bank_sum = stats.tile([P, 4], F32, tag="bank_sum")
            stat_tiles[b] = (bank_max, neg_max, bank_sum)

        def bank_maximum(b, h, c):
            bank_max, neg_max, bank_sum = stat_tiles[b]
            sc, first, width = score_banks[(b, h)][c]
            nc.vector.tensor_reduce(
                out=bank_max[:, 2 * h + c : 2 * h + c + 1], in_=sc, axis=AXIS_X, op=ALU.max
            )

        def maxima_of_both_heads(b):
            bank_max, neg_max, bank_sum = stat_tiles[b]
            keys = (b + 1) * P
            nc.vector.tensor_reduce(
                out=bank_max[:, 0:4:2],
                in_=turned[("scores", b)][:, 0 : 2 * keys].rearrange("p (h k) -> p h k", h=2),
                axis=AXIS_X,
                op=ALU.max,
            )

        def negative_maximum(b, h):
            bank_max, neg_max, bank_sum = stat_tiles[b]
            if key_passes_of[b] == 1:
                nc.vector.tensor_scalar(
                    out=neg_max[:, h : h + 1],
                    in0=bank_max[:, 2 * h : 2 * h + 1],
                    scalar1=-SCALE,
                    scalar2=None,
                    op0=ALU.mult,
                )
                return
            nc.vector.tensor_scalar(
                out=neg_max[:, h : h + 1],
                in0=bank_max[:, 2 * h : 2 * h + 1],
                scalar1=bank_max[:, 2 * h + 1 : 2 * h + 2],
                scalar2=-SCALE,
                op0=ALU.max,
                op1=ALU.mult,
            )

        def negative_maxima(b):
            bank_max, neg_max, bank_sum = stat_tiles[b]
            nc.vector.tensor_scalar(
                out=neg_max[:],
                in0=bank_max[:, 0:4:2],
                scalar1=-SCALE,
                scalar2=None,
                op0=ALU.mult,
            )

        def exps(b, h):
            if b not in exp_tiles:
                expd = work.tile([P, 2 * T], F32, tag="expd")
                exp_tiles[b] = expd
            bank_max, neg_max, bank_sum = stat_tiles[b]
            for c, (sc, first, width) in enumerate(score_banks[(b, h)]):
                nc.scalar.activation(
                    out=exp_tiles[b][:, h * T + first : h * T + first + width],
                    in_=sc,
                    func=ACT.Exp,
                    bias=neg_max[:, h : h + 1],
                    scale=SCALE,
                    accum_out=bank_sum[:, 2 * h + c : 2 * h + c + 1],
                )

        def row_sums(b):
            bank_max, neg_max, bank_sum = stat_tiles[b]
            row_sum = stats.tile([P, 2], F32, tag="row_sum")
            row_sum_tiles[b] = row_sum
            nc.vector.tensor_reduce(
                out=row_sum[:],
                in_=bank_sum[:].rearrange("p (h c) -> p h c", c=2),
                axis=AXIS_X,
                op=ALU.add,
            )

        def inverse_sums(b):
            bank_max, neg_max, bank_sum = stat_tiles[b]
            inv_sum = stats.tile([P, 2], F32, tag="inv_sum")
            inv_sums[b] = inv_sum
            if key_passes_of[b] == 1:
                nc.vector.reciprocal(out=inv_sum[:], in_=bank_sum[:, 0:4:2])
            else:
                nc.vector.reciprocal(out=inv_sum[:], in_=row_sum_tiles[b][:])

        def scale_second(b):
            keys = (b + 1) * P
            second = work.tile([P, T], F32, tag="second")
            seconds[b] = second
            nc.vector.tensor_scalar(
                out=second[:, 0:keys],
                in0=exp_tiles[b][:, T : T + keys],
                scalar1=inv_sums[b][:, 1:2],
                scalar2=neg_lam[:, 0:1],
                op0=ALU.mult,
                op1=ALU.mult,
            )

        def combine(b):
            keys = (b + 1) * P
            nc.vector.scalar_tensor_tensor(
                out=att[b][:, 0:keys],
                in0=exp_tiles[b][:, 0:keys],
                scalar=inv_sums[b][:, 0:1],
                in1=seconds[b][:, 0:keys],
                op0=ALU.mult,
                op1=ALU.add,
            )

        def transpose_att(b):
            att_words = att[b][:].bitcast(F32)
            at = psum_t.tile([P, BANK], F32, tag="tp")
            turned[("att", b)] = at
            for i in range(key_passes_of[b] * 2):
                nc.tensor.transpose(
                    at[:, i * P : (i + 1) * P], att_words[:, i * P : (i + 1) * P], ident_f32[:]
                )

        def regroup_att(b):
            g = key_passes_of[b]
            nc.scalar.copy(
                out=att_grouped[b][:].bitcast(F32).rearrange("p (g n u) -> p g n u", g=g, u=2),
                in_=turned[("att", b)][:, 0 : g * 2 * P].rearrange("p (g u n) -> p g n u", g=g, u=2),
            )

        def quantise_att(b):
            nc.vector.quantize_mx(
                out=att_codes[b][:].bitcast(FP8X4), scales=att_scales[b][:], in_=att_grouped[b][:]
            )

        def attention_output(b, pool, tag):
            acc = pool.tile([P, BANK], F32, tag=tag)
            turned[("out", b)] = acc
            for g in range(key_passes_of[b]):
                nc.tensor.matmul_mx(
                    out=acc[:, 0:H],
                    lhsT=att_codes[b][:, g * P : (g + 1) * P].bitcast(FP8X4),
                    lhsT_scale=att_scales[b][:, g * P : (g + 1) * P],
                    rhs=v_codes[:, g * H : (g + 1) * H].bitcast(FP8X4),
                    rhs_scale=v_scales[:, g * H : (g + 1) * H],
                    start=(g == 0),
                    stop=(g == key_passes_of[b] - 1),
                )

        def store_output(b, copy):
            o_sb = keep.tile([P, H], F32, name="o_sb%d" % b)
            copy(out=o_sb[:], in_=turned[("out", b)][:, 0:H])
            nc.sync.dma_start(out=out_rows[b * P : (b + 1) * P, :], in_=o_sb[:])

        on_vector = nc.vector.tensor_copy
        on_scalar = nc.scalar.copy
        ORDER = [3, 7, 6, 5, 4, 2, 1, 0]

        def regroup_unit(n, copy):
            regroup_words(n // C_PASSES, n % C_PASSES, copy)

        for b in ORDER:
            row_statistics(b)

        idle = psum_s.tile([P, BANK], F32, tag="sc")
        keep_busy(idle)
        keep_busy(idle)
        keep_busy(idle)

        transpose_queries(1)
        transpose_keys(0, 0)
        transpose_keys(0, 1)
        transpose_queries(3)
        keep_busy(idle)
        copy_queries(1)
        copy_keys(0, 0, on_vector)
        copy_keys(0, 1, on_vector)
        scores(3, 0)
        scores(3, 1)
        copy_queries(3)
        transpose_keys(1, 0)
        lam_transpose()
        transpose_keys(1, 1)
        keep_busy(idle)
        bank_maximum(3, 0, 0)
        bank_maximum(3, 1, 0)
        negative_maximum(3, 0)
        negative_maximum(3, 1)
        copy_keys(1, 0, on_scalar)
        copy_keys(1, 1, on_scalar)
        lam_columns()
        exps(3, 0)
        exps(3, 1)
        lam_products()
        scores(7, 0)
        lam_sums()
        lam_exps()
        scores(7, 1)
        for c_pass in range(C_PASSES):
            words_onto_partitions(0, c_pass)

        bank_maximum(7, 0, 0)
        bank_maximum(7, 0, 1)
        inverse_sums(3)
        lam_negative()
        negative_maximum(7, 0)
        scale_second(3)
        bank_maximum(7, 1, 0)
        bank_maximum(7, 1, 1)
        combine(3)
        negative_maximum(7, 1)
        exps(7, 0)
        scores(6, 0)
        regroup_unit(0, on_scalar)
        regroup_unit(1, on_scalar)
        regroup_unit(2, on_vector)
        regroup_unit(3, on_vector)
        words_onto_partitions(1, 0)
        transpose_att(3)
        exps(7, 1)
        scores(6, 1)
        regroup_unit(4, on_scalar)
        transpose_queries(2)
        for c_pass in range(1, C_PASSES):
            words_onto_partitions(1, c_pass)
        regroup_att(3)
        copy_queries(2)

        for step in range(2, 5):
            before, last, cur, nxt = ORDER[step - 2 : step + 2]
            piece = step
            unit = 4 * step - 3
            bank_maximum(cur, 0, 0)
            bank_maximum(cur, 0, 1)
            row_sums(last)
            bank_maximum(cur, 1, 0)
            negative_maximum(cur, 0)
            inverse_sums(last)
            bank_maximum(cur, 1, 1)
            scale_second(last)
            quantise_att(before)
            negative_maximum(cur, 1)
            combine(last)
            quantise_piece(piece - 2)

            exps(cur, 0)
            scores(nxt, 0)
            regroup_unit(unit, on_scalar)
            regroup_unit(unit + 1, on_scalar)
            words_onto_partitions(piece, 0)
            transpose_att(last)
            exps(cur, 1)
            scores(nxt, 1)
            regroup_unit(unit + 2, on_scalar)
            regroup_unit(unit + 3, on_scalar)
            for c_pass in range(1, C_PASSES):
                words_onto_partitions(piece, c_pass)
            regroup_att(last)

        bank_maximum(2, 0, 0)
        row_sums(4)
        bank_maximum(2, 1, 0)
        inverse_sums(4)
        quantise_piece(3)
        negative_maxima(2)
        scale_second(4)
        quantise_att(5)
        project_v(0, 0, psum_s, "sc")
        transpose_queries(0)
        project_v(0, 1, psum_s, "sc")
        for n in range(17, 20):
            regroup_unit(n, on_scalar)
        regroup_v(0, 0)
        copy_queries(0)
        exps(2, 0)
        exps(2, 1)
        regroup_v(0, 1)
        quantise_piece(4)
        combine(4)
        scores_of_both_heads(1)
        scores_of_both_heads(0)
        project_v(1, 0, psum_t, "tp")
        transpose_att(4)
        maxima_of_both_heads(1)
        inverse_sums(2)
        quantise_v(0)
        negative_maxima(1)
        scale_second(2)
        maxima_of_both_heads(0)
        combine(2)
        negative_maxima(0)
        exps(1, 0)
        exps(1, 1)
        exps(0, 0)
        exps(0, 1)
        regroup_v(1, 0)
        regroup_att(4)
        transpose_att(2)
        project_v(1, 1, psum_t, "tp")
        inverse_sums(1)
        inverse_sums(0)
        scale_second(1)
        scale_second(0)
        combine(1)
        quantise_att(4)
        combine(0)
        regroup_att(2)
        regroup_v(1, 1)
        attention_output(3, psum_t, "tp")
        transpose_att(1)
        regroup_att(1)
        transpose_att(0)
        quantise_att(2)
        attention_output(2, psum_t, "tp")
        store_output(3, on_vector)
        quantise_v(1)
        regroup_att(0)
        quantise_att(1)
        quantise_att(0)
        for b in (7, 6, 5, 4):
            attention_output(b, psum_s, "sc")
        attention_output(1, psum_t, "tp")
        attention_output(0, psum_t, "tp")
        store_output(2, on_scalar)
        for b, copy in ((7, on_scalar), (6, on_vector), (5, on_scalar), (4, on_vector)):
            store_output(b, copy)
        store_output(1, on_vector)
        store_output(0, on_scalar)
